import numpy as np
import ml_dtypes


def mxq(x, axis, fmt="e4m3"):
    dtype, down = {"e4m3": (ml_dtypes.float8_e4m3fn, 7), "e5m2": (ml_dtypes.float8_e5m2, 14)}[fmt]
    v = np.moveaxis(np.asarray(x, np.float32).astype(ml_dtypes.bfloat16).astype(np.float64), axis, -1)
    blocks = v.reshape(v.shape[:-1] + (-1, 32))
    amax = np.abs(blocks).max(-1, keepdims=True)
    byte = np.maximum(np.where(amax > 0, np.frexp(amax)[1] - 1 + 127, 0) - down, 1)
    scale = np.exp2(byte - 127.0)
    codes = (blocks / scale).astype(np.float32).astype(dtype).astype(np.float64)
    return np.moveaxis((codes * scale).reshape(v.shape), -1, axis)


WIDE = False


def mx_kscale(k):
    if not WIDE:
        return np.ones(k)
    levels = np.array([10, -10, 5, -5, 0])
    a = np.random.permutation(np.resize(levels, k // 512 * 4)).reshape(k // 512, 4)
    idx = np.arange(k)
    return np.exp2(a[idx // 512, idx % 128 // 32])


BF16 = ml_dtypes.bfloat16


def bf(x):
    return np.asarray(x, np.float32).astype(BF16)


def f64(x):
    return np.asarray(x).astype(np.float64)


B, R, U, HID, G = 4096, 256, 512, 512, 1024
F = 2 * R + U
GAMMA_MAX = 2.0


def sigmoid(v):
    return 1.0 / (1.0 + np.exp(-v))


def setup_inputs():
    s = mx_kscale(U)
    w1 = np.random.standard_normal((HID, F)) / np.sqrt(F)
    w1[:, 2 * R:] /= s
    return {"y_tilde": bf(np.random.standard_normal((B, R))),
            "z_tilde": bf(np.random.standard_normal((B, R))),
            "u": bf(np.random.standard_normal((B, U)) * s),
            "dt": bf(0.3 + 0.2 * np.random.random(1)),
            "omega_sq": bf(1.0 + 0.1 * np.random.standard_normal(R)),
            "alpha_lambda": bf(-np.random.random(R) * 0.5),
            "B_tilde": bf(np.random.standard_normal((R, U)) / np.sqrt(U) / s),
            "dmlp_w1": bf(w1),
            "dmlp_b1": bf(np.random.standard_normal(HID) * 0.3),
            "dmlp_w2": bf(np.random.standard_normal((R, HID)) * 2.0 / np.sqrt(HID)),
            "dmlp_b2": bf(np.random.standard_normal(R) * 0.5)}


def reference(y_tilde, z_tilde, u, dt, omega_sq, alpha_lambda, B_tilde, dmlp_w1, dmlp_b1, dmlp_w2, dmlp_b2):
    y, z, step = f64(y_tilde), f64(z_tilde), f64(dt)
    fq = mxq(np.concatenate([y, z, f64(u)], axis=-1), 1, "e4m3")
    b_dot_u = fq[:, 2 * R:] @ mxq(f64(B_tilde), 1, "e4m3").T
    h = np.tanh((fq @ mxq(f64(dmlp_w1), 1, "e4m3").T) + f64(dmlp_b1))
    gamma_tilde = GAMMA_MAX * sigmoid((mxq(h, 1, "e4m3") @ mxq(f64(dmlp_w2), 1, "e4m3").T) + f64(dmlp_b2))
    z_next = z + step * (b_dot_u - (f64(omega_sq) - f64(alpha_lambda)) * y - gamma_tilde * z)
    y_next = y + step * z_next
    return z_next, gamma_tilde, y_next

@@ -1,0 +1,277 @@
+import concourse.mybir as mybir
+from concourse.masks import make_identity
+
+F32 = mybir.dt.float32
+BF16 = mybir.dt.bfloat16
+U32 = mybir.dt.uint32
+U8 = mybir.dt.uint8
+FP8X4 = mybir.dt.float8_e4m3fn_x4
+ACT = mybir.ActivationFunctionType
+ALU = mybir.AluOpType
+
+P = 128
+PACK = 4
+BATCH, MODES, DRIVE, HIDDEN = 4096, 256, 512, 512
+N_TILES = BATCH // P
+CHUNK_TILES = 4
+CHUNK = CHUNK_TILES * P
+N_CHUNKS = N_TILES // CHUNK_TILES
+FEAT_PASSES = 2
+HID_TILES = HIDDEN // P
+MODE_TILES = MODES // P
+PAIR = 2
+
+FLOPS = 2 * BATCH * (2 * MODES + DRIVE) * HIDDEN + 2 * BATCH * HIDDEN * MODES + 2 * BATCH * DRIVE * MODES
+
+
+def tile_instrumentedlocmblock_pa_t_kernel(
+    tc, y_tilde, z_tilde, u, dt, omega_sq, alpha_lambda, B_tilde, dmlp_w1, dmlp_b1, dmlp_w2, dmlp_b2,
+    out_0, out_1, out_2,
+):
+    nc = tc.nc
+
+    y_rows = y_tilde.rearrange("(p t) m -> p t m", t=N_TILES)
+    z_rows = z_tilde.rearrange("(p t) m -> p t m", t=N_TILES)
+    u_rows = u.rearrange("(p t) k -> p t k", t=N_TILES)
+    z_next_rows = out_0.rearrange("(p t) m -> p t m", t=N_TILES)
+    gamma_rows = out_1.rearrange("(p t) m -> p t m", t=N_TILES)
+    y_next_rows = out_2.rearrange("(p t) m -> p t m", t=N_TILES)
+
+    with tc.tile_pool(name="consts", bufs=1) as consts, \
+            tc.tile_pool(name="inputs", bufs=N_CHUNKS) as inputs, \
+            tc.tile_pool(name="work", bufs=2) as work, \
+            tc.psum_pool(name="psum", bufs=1) as psum:
+
+        w1_sb = consts.tile([P, HID_TILES, 2 * MODES + DRIVE], BF16)
+        nc.sync.dma_start(out=w1_sb[:], in_=dmlp_w1.rearrange("(j p) k -> p j k", p=P))
+
+        y_sb, z_sb, u_sb = {}, {}, {}
+
+        def load_chunk(c):
+            tiles = slice(c * CHUNK_TILES, (c + 1) * CHUNK_TILES)
+            y_sb[c] = inputs.tile([P, CHUNK_TILES, MODES], BF16, name="y_sb", tag="y")
+            z_sb[c] = inputs.tile([P, CHUNK_TILES, MODES], BF16, name="z_sb", tag="z")
+            u_sb[c] = inputs.tile([P, CHUNK_TILES, DRIVE], BF16, name="u_sb", tag="u")
+            nc.sync.dma_start(out=y_sb[c][:], in_=y_rows[:, tiles, :])
+            nc.sync.dma_start(out=z_sb[c][:], in_=z_rows[:, tiles, :])
+            nc.sync.dma_start(out=u_sb[c][:], in_=u_rows[:, tiles, :])
+
+        load_chunk(0)
+
+        bias_rows = consts.tile([P, P], BF16)
+        nc.vector.memset(bias_rows[:], 0.0)
+        nc.sync.dma_start(out=bias_rows[0:HID_TILES, :], in_=dmlp_b1.rearrange("(j p) -> j p", p=P))
+        nc.sync.dma_start(
+            out=bias_rows[HID_TILES:HID_TILES + MODE_TILES, :], in_=dmlp_b2.rearrange("(m p) -> m p", p=P)
+        )
+        bt_sb = consts.tile([P, MODE_TILES, DRIVE], BF16)
+        nc.sync.dma_start(out=bt_sb[:], in_=B_tilde.rearrange("(m p) k -> p m k", p=P))
+        w2_sb = consts.tile([P, MODE_TILES, HIDDEN], BF16)
+        nc.sync.dma_start(out=w2_sb[:], in_=dmlp_w2.rearrange("(m p) k -> p m k", p=P))
+        load_chunk(1)
+        omega_bc = consts.tile([P, MODES], BF16)
+        nc.sync.dma_start(out=omega_bc[:], in_=omega_sq.partition_broadcast(P))
+        alpha_bc = consts.tile([P, MODES], BF16)
+        nc.sync.dma_start(out=alpha_bc[:], in_=alpha_lambda.partition_broadcast(P))
+        dt_bf = consts.tile([P, 1], BF16)
+        nc.sync.dma_start(out=dt_bf[:], in_=dt.partition_broadcast(P))
+        for c in range(2, N_CHUNKS):
+            load_chunk(c)
+
+        ident_f32 = consts.tile([P, P], F32)
+        make_identity(nc, ident_f32[:])
+        ident_bf = consts.tile([P, P], BF16)
+        make_identity(nc, ident_bf[:])
+
+        def words_to_partitions(word_blocks, grouped_words, copy):
+            bank = psum.tile([P, len(word_blocks), P], F32, name="bank", tag="tp", bufs=2)
+            for q, block in enumerate(word_blocks):
+                nc.tensor.transpose(bank[:, q, :], block, ident_f32[:])
+            copy(out=grouped_words, in_=bank[:].rearrange("p (g h) r -> p g r h", h=2))
+
+        w1_grouped = consts.tile([P, FEAT_PASSES, HIDDEN, PACK], BF16, align_bytes=64)
+        w1_codes = consts.tile([P, FEAT_PASSES, HIDDEN], U32, align_bytes=64)
+        w1_scales = consts.tile([P, FEAT_PASSES, HIDDEN], U8, align_bytes=64)
+        for j in range(HID_TILES):
+            words = w1_sb[:, j, :].bitcast(F32)
+            words_to_partitions(
+                [words[:, q * P:(q + 1) * P] for q in range(2 * FEAT_PASSES)],
+                w1_grouped[:].bitcast(F32)[:, :, j * P:(j + 1) * P, :],
+                nc.vector.tensor_copy,
+            )
+        nc.vector.quantize_mx(
+            out=w1_codes[:].rearrange("p g r -> p (g r)").bitcast(FP8X4),
+            scales=w1_scales[:].rearrange("p g r -> p (g r)"),
+            in_=w1_grouped[:].rearrange("p g r t -> p (g r t)"),
+        )
+
+        f_codes, f_scales = {}, {}
+
+        def front(c):
+            grouped = work.tile([P, FEAT_PASSES, CHUNK, PACK], BF16, name="f_grouped", tag="f_grouped", align_bytes=64)
+            for t in range(CHUNK_TILES):
+                u_words = u_sb[c][:, t, :].bitcast(F32)
+                words_to_partitions(
+                    [y_sb[c][:, t, :].bitcast(F32), z_sb[c][:, t, :].bitcast(F32), u_words[:, 0:P], u_words[:, P:2 * P]],
+                    grouped[:].bitcast(F32)[:, :, t * P:(t + 1) * P, :],
+                    nc.scalar.copy,
+                )
+            f_codes[c] = work.tile([P, FEAT_PASSES, CHUNK], U32, name="f_codes", tag="f_codes", align_bytes=64, bufs=3)
+            f_scales[c] = work.tile([P, FEAT_PASSES, CHUNK], U8, name="f_scales", tag="f_scales", align_bytes=64, bufs=3)
+            nc.vector.quantize_mx(
+                out=f_codes[c][:].rearrange("p g r -> p (g r)").bitcast(FP8X4),
+                scales=f_scales[c][:].rearrange("p g r -> p (g r)"),
+                in_=grouped[:].rearrange("p g r t -> p (g r t)"),
+            )
+
+        front(0)
+
+        bt_grouped = consts.tile([P, 1, MODES, PACK], BF16, align_bytes=64)
+        bt_codes = consts.tile([P, MODES], U32, align_bytes=64)
+        bt_scales = consts.tile([P, MODES], U8, align_bytes=64)
+        for m in range(MODE_TILES):
+            words = bt_sb[:, m, :].bitcast(F32)
+            words_to_partitions(
+                [words[:, 0:P], words[:, P:2 * P]],
+                bt_grouped[:].bitcast(F32)[:, :, m * P:(m + 1) * P, :],
+                nc.vector.tensor_copy,
+            )
+        nc.vector.quantize_mx(
+            out=bt_codes[:].bitcast(FP8X4),
+            scales=bt_scales[:],
+            in_=bt_grouped[:].rearrange("p g r t -> p (g r t)"),
+        )
+
+        w2_grouped = consts.tile([P, MODES, PACK], BF16, align_bytes=64)
+        w2_codes = consts.tile([P, MODES], U32, align_bytes=64)
+        w2_scales = consts.tile([P, MODES], U8, align_bytes=64)
+        for m in range(MODE_TILES):
+            bank = psum.tile([P, HID_TILES, P], BF16, name="bank", tag="tp", bufs=2)
+            for j in range(HID_TILES):
+                nc.tensor.transpose(bank[:, j, :], w2_sb[:, m, j * P:(j + 1) * P], ident_bf[:])
+            nc.vector.tensor_copy(
+                out=w2_grouped[:, m * P:(m + 1) * P, :], in_=bank[:].rearrange("p j r -> p r j")
+            )
+        nc.vector.quantize_mx(
+            out=w2_codes[:].bitcast(FP8X4),
+            scales=w2_scales[:],
+            in_=w2_grouped[:].rearrange("p r j -> p (r j)"),
+        )
+
+        bank = psum.tile([P, P], BF16, name="bank", tag="tp", bufs=2)
+        nc.tensor.transpose(bank[:], bias_rows[:], ident_bf[:])
+        b1_col = consts.tile([P, HID_TILES], F32)
+        nc.vector.tensor_copy(out=b1_col[:], in_=bank[:, 0:HID_TILES])
+        half_b2_col = consts.tile([P, MODE_TILES], F32)
+        nc.vector.tensor_scalar_mul(out=half_b2_col[:], in0=bank[:, HID_TILES:HID_TILES + MODE_TILES], scalar1=0.5)
+
+        dt_col = consts.tile([P, 1], F32)
+        nc.vector.tensor_copy(out=dt_col[:], in_=dt_bf[:])
+        neg_dt_col = consts.tile([P, 1], F32)
+        nc.vector.tensor_scalar_mul(out=neg_dt_col[:], in0=dt_col[:], scalar1=-1.0)
+        stiff_bc = consts.tile([P, MODES], F32)
+        nc.vector.tensor_tensor(out=stiff_bc[:], in0=omega_bc[:], in1=alpha_bc[:], op=ALU.subtract)
+        dt_stiff_bc = consts.tile([P, MODES], F32)
+        nc.vector.tensor_scalar_mul(out=dt_stiff_bc[:], in0=stiff_bc[:], scalar1=dt_col[:, 0:1])
+
+        h_codes, h_scales, forced = {}, {}, {}
+
+        def hidden(c):
+            h_planes = work.tile([P, HID_TILES, CHUNK], BF16, name="h_planes", tag="h_planes")
+            for j in range(HID_TILES):
+                cols = slice(j * P, (j + 1) * P)
+                acc = psum.tile([P, CHUNK], F32, name="h_acc", tag="h", bufs=2)
+                for g in range(FEAT_PASSES):
+                    nc.tensor.matmul_mx(
+                        out=acc[:],
+                        lhsT=w1_codes[:, g, cols].bitcast(FP8X4),
+                        lhsT_scale=w1_scales[:, g, cols],
+                        rhs=f_codes[c][:, g, :].bitcast(FP8X4),
+                        rhs_scale=f_scales[c][:, g, :],
+                        start=(g == 0),
+                        stop=(g == FEAT_PASSES - 1),
+                    )
+                nc.scalar.activation(out=h_planes[:, j, :], in_=acc[:], func=ACT.Tanh, bias=b1_col[:, j:j + 1], scale=1.0)
+            h_grouped = work.tile([P, CHUNK, PACK], BF16, name="h_grouped", tag="h_grouped", align_bytes=64)
+            nc.vector.tensor_copy(
+                out=h_grouped[:].rearrange("p (c i) j -> p c j i", i=4),
+                in_=h_planes[:].rearrange("p j (c i) -> p c j i", i=4),
+            )
+            h_codes[c] = work.tile([P, CHUNK], U32, name="h_codes", tag="h_codes", align_bytes=64)
+            h_scales[c] = work.tile([P, CHUNK], U8, name="h_scales", tag="h_scales", align_bytes=64)
+            nc.vector.quantize_mx(
+                out=h_codes[c][:].bitcast(FP8X4),
+                scales=h_scales[c][:],
+                in_=h_grouped[:].rearrange("p r j -> p (r j)"),
+            )
+
+        def drive(c):
+            spring = work.tile([P, CHUNK_TILES, MODES], F32, name="spring", tag="spring")
+            nc.vector.tensor_tensor(
+                out=spring[:], in0=y_sb[c][:],
+                in1=dt_stiff_bc[:].unsqueeze(1).to_broadcast([P, CHUNK_TILES, MODES]), op=ALU.mult,
+            )
+            forced[c] = work.tile([P, CHUNK_TILES, MODES], F32, name="forced", tag="forced")
+            for s in range(CHUNK_TILES // PAIR):
+                bu = psum.tile([P, PAIR, MODES], F32, name="bu", tag="bu", bufs=1)
+                for i in range(PAIR):
+                    cols = slice((s * PAIR + i) * P, (s * PAIR + i + 1) * P)
+                    nc.tensor.matmul_mx(
+                        out=bu[:, i, :],
+                        lhsT=f_codes[c][:, 1, cols].bitcast(FP8X4),
+                        lhsT_scale=f_scales[c][:, 1, cols],
+                        rhs=bt_codes[:].bitcast(FP8X4),
+                        rhs_scale=bt_scales[:],
+                        start=True,
+                        stop=True,
+                    )
+                pair = slice(s * PAIR, (s + 1) * PAIR)
+                nc.vector.scalar_tensor_tensor(
+                    out=forced[c][:, pair, :], in0=bu[:], scalar=dt_col[:, 0:1], in1=spring[:, pair, :],
+                    op0=ALU.mult, op1=ALU.subtract,
+                )
+
+        def damping_and_step(c):
+            th_t = work.tile([P, MODE_TILES, CHUNK], F32, name="th_t", tag="th_t")
+            for m in range(MODE_TILES):
+                cols = slice(m * P, (m + 1) * P)
+                acc = psum.tile([P, CHUNK], F32, name="g_acc", tag="g", bufs=2)
+                nc.tensor.matmul_mx(
+                    out=acc[:],
+                    lhsT=w2_codes[:, cols].bitcast(FP8X4),
+                    lhsT_scale=w2_scales[:, cols],
+                    rhs=h_codes[c][:].bitcast(FP8X4),
+                    rhs_scale=h_scales[c][:],
+                    start=True,
+                    stop=True,
+                )
+                nc.scalar.activation(out=th_t[:, m, :], in_=acc[:], func=ACT.Tanh, bias=half_b2_col[:, m:m + 1], scale=0.5)
+            gamma = work.tile([P, CHUNK_TILES, MODES], F32, name="gamma", tag="gamma")
+            for s in range(CHUNK_TILES // PAIR):
+                th = psum.tile([P, PAIR, MODES], F32, name="th", tag="th", bufs=1)
+                for i in range(PAIR):
+                    t = s * PAIR + i
+                    for m in range(MODE_TILES):
+                        nc.tensor.transpose(th[:, i, m * P:(m + 1) * P], th_t[:, m, t * P:(t + 1) * P], ident_f32[:])
+                nc.scalar.activation(out=gamma[:, s * PAIR:(s + 1) * PAIR, :], in_=th[:], func=ACT.Identity, bias=1.0, scale=1.0)
+            tiles = slice(c * CHUNK_TILES, (c + 1) * CHUNK_TILES)
+            nc.sync.dma_start(out=gamma_rows[:, tiles, :], in_=gamma[:])
+            keep = work.tile([P, CHUNK_TILES, MODES], F32, name="keep", tag="keep")
+            nc.scalar.activation(out=keep[:], in_=gamma[:], func=ACT.Identity, bias=1.0, scale=neg_dt_col[:, 0:1])
+            damped = work.tile([P, CHUNK_TILES, MODES], F32, name="damped", tag="damped")
+            nc.vector.tensor_tensor(out=damped[:], in0=keep[:], in1=z_sb[c][:], op=ALU.mult)
+            z_next = work.tile([P, CHUNK_TILES, MODES], F32, name="z_next", tag="z_next")
+            nc.vector.tensor_tensor(out=z_next[:], in0=damped[:], in1=forced[c][:], op=ALU.add)
+            nc.sync.dma_start(out=z_next_rows[:, tiles, :], in_=z_next[:])
+            y_next = work.tile([P, CHUNK_TILES, MODES], F32, name="y_next", tag="y_next")
+            nc.vector.scalar_tensor_tensor(
+                out=y_next[:], in0=z_next[:], scalar=dt_col[:, 0:1], in1=y_sb[c][:], op0=ALU.mult, op1=ALU.add,
+            )
+            nc.sync.dma_start(out=y_next_rows[:, tiles, :], in_=y_next[:])
+
+        for c in range(N_CHUNKS):
+            if c + 1 < N_CHUNKS:
+                front(c + 1)
+            hidden(c)
+            drive(c)
+            damping_and_step(c)

@@ -20,6 +20,7 @@ FEAT_PASSES = 2
 HID_TILES = HIDDEN // P
 MODE_TILES = MODES // P
 PAIR = 2
+RING_BANKS = 6
 
 FLOPS = 2 * BATCH * (2 * MODES + DRIVE) * HIDDEN + 2 * BATCH * HIDDEN * MODES + 2 * BATCH * DRIVE * MODES
 
@@ -37,27 +38,39 @@ def tile_instrumentedlocmblock_pa_t_kernel(
     gamma_rows = out_1.rearrange("(p t) m -> p t m", t=N_TILES)
     y_next_rows = out_2.rearrange("(p t) m -> p t m", t=N_TILES)
 
+    def chunk_tiles(c):
+        return slice(c * CHUNK_TILES, (c + 1) * CHUNK_TILES)
+
     with tc.tile_pool(name="consts", bufs=1) as consts, \
             tc.tile_pool(name="inputs", bufs=N_CHUNKS) as inputs, \
             tc.tile_pool(name="work", bufs=2) as work, \
-            tc.psum_pool(name="psum", bufs=1) as psum:
+            tc.psum_pool(name="psum", bufs=1) as psum, \
+            tc.manual_schedule():
 
-        w1_sb = consts.tile([P, HID_TILES, 2 * MODES + DRIVE], BF16)
-        nc.sync.dma_start(out=w1_sb[:], in_=dmlp_w1.rearrange("(j p) k -> p j k", p=P))
+        warm = consts.tile([P, 1], F32)
+        nc.vector.memset(warm[:], 0.0)
+        nc.scalar.activation(out=warm[:], in_=warm[:], func=ACT.Tanh)
+
+        ident_f32 = consts.tile([P, P], F32)
+        make_identity(nc, ident_f32[:])
+        ident_bf = consts.tile([P, P], BF16)
+        make_identity(nc, ident_bf[:])
 
         y_sb, z_sb, u_sb = {}, {}, {}
 
         def load_chunk(c):
-            tiles = slice(c * CHUNK_TILES, (c + 1) * CHUNK_TILES)
             y_sb[c] = inputs.tile([P, CHUNK_TILES, MODES], BF16, name="y_sb", tag="y")
             z_sb[c] = inputs.tile([P, CHUNK_TILES, MODES], BF16, name="z_sb", tag="z")
             u_sb[c] = inputs.tile([P, CHUNK_TILES, DRIVE], BF16, name="u_sb", tag="u")
-            nc.sync.dma_start(out=y_sb[c][:], in_=y_rows[:, tiles, :])
-            nc.sync.dma_start(out=z_sb[c][:], in_=z_rows[:, tiles, :])
-            nc.sync.dma_start(out=u_sb[c][:], in_=u_rows[:, tiles, :])
+            nc.sync.dma_start(out=y_sb[c][:], in_=y_rows[:, chunk_tiles(c), :])
+            nc.sync.dma_start(out=z_sb[c][:], in_=z_rows[:, chunk_tiles(c), :])
+            nc.sync.dma_start(out=u_sb[c][:], in_=u_rows[:, chunk_tiles(c), :])
 
         load_chunk(0)
-
+        w1_sb = consts.tile([P, HID_TILES, 2 * MODES + DRIVE], BF16)
+        w1_rows = dmlp_w1.rearrange("(j p) k -> p j k", p=P)
+        for j in range(HID_TILES):
+            nc.sync.dma_start(out=w1_sb[:, j, :], in_=w1_rows[:, j, :])
         bias_rows = consts.tile([P, P], BF16)
         nc.vector.memset(bias_rows[:], 0.0)
         nc.sync.dma_start(out=bias_rows[0:HID_TILES, :], in_=dmlp_b1.rearrange("(j p) -> j p", p=P))
@@ -66,9 +79,9 @@ def tile_instrumentedlocmblock_pa_t_kernel(
         )
         bt_sb = consts.tile([P, MODE_TILES, DRIVE], BF16)
         nc.sync.dma_start(out=bt_sb[:], in_=B_tilde.rearrange("(m p) k -> p m k", p=P))
+        load_chunk(1)
         w2_sb = consts.tile([P, MODE_TILES, HIDDEN], BF16)
         nc.sync.dma_start(out=w2_sb[:], in_=dmlp_w2.rearrange("(m p) k -> p m k", p=P))
-        load_chunk(1)
         omega_bc = consts.tile([P, MODES], BF16)
         nc.sync.dma_start(out=omega_bc[:], in_=omega_sq.partition_broadcast(P))
         alpha_bc = consts.tile([P, MODES], BF16)
@@ -78,53 +91,174 @@ def tile_instrumentedlocmblock_pa_t_kernel(
         for c in range(2, N_CHUNKS):
             load_chunk(c)
 
-        ident_f32 = consts.tile([P, P], F32)
-        make_identity(nc, ident_f32[:])
-        ident_bf = consts.tile([P, P], BF16)
-        make_identity(nc, ident_bf[:])
+        def ring_bank(shape, dtype):
+            return psum.tile(shape, dtype, name="ring", tag="ring", bufs=RING_BANKS)
 
         def words_to_partitions(word_blocks, grouped_words, copy):
-            bank = psum.tile([P, len(word_blocks), P], F32, name="bank", tag="tp", bufs=2)
+            bank = ring_bank([P, len(word_blocks), P], F32)
             for q, block in enumerate(word_blocks):
                 nc.tensor.transpose(bank[:, q, :], block, ident_f32[:])
             copy(out=grouped_words, in_=bank[:].rearrange("p (g h) r -> p g r h", h=2))
 
-        w1_grouped = consts.tile([P, FEAT_PASSES, HIDDEN, PACK], BF16, align_bytes=64)
-        w1_codes = consts.tile([P, FEAT_PASSES, HIDDEN], U32, align_bytes=64)
-        w1_scales = consts.tile([P, FEAT_PASSES, HIDDEN], U8, align_bytes=64)
-        for j in range(HID_TILES):
-            words = w1_sb[:, j, :].bitcast(F32)
-            words_to_partitions(
-                [words[:, q * P:(q + 1) * P] for q in range(2 * FEAT_PASSES)],
-                w1_grouped[:].bitcast(F32)[:, :, j * P:(j + 1) * P, :],
-                nc.vector.tensor_copy,
-            )
-        nc.vector.quantize_mx(
-            out=w1_codes[:].rearrange("p g r -> p (g r)").bitcast(FP8X4),
-            scales=w1_scales[:].rearrange("p g r -> p (g r)"),
-            in_=w1_grouped[:].rearrange("p g r t -> p (g r t)"),
-        )
+        f_grouped, f_codes, f_scales = {}, {}, {}
+        h_planes, h_grouped, h_codes, h_scales = {}, {}, {}, {}
+        bu, spring, forced, th_t, keep, damped, z_next = {}, {}, {}, {}, {}, {}, {}
 
-        f_codes, f_scales = {}, {}
-
-        def front(c):
-            grouped = work.tile([P, FEAT_PASSES, CHUNK, PACK], BF16, name="f_grouped", tag="f_grouped", align_bytes=64)
+        def transpose_features(c):
+            f_grouped[c] = work.tile([P, FEAT_PASSES, CHUNK, PACK], BF16, name="f_grouped", tag="f_grouped", align_bytes=64)
             for t in range(CHUNK_TILES):
                 u_words = u_sb[c][:, t, :].bitcast(F32)
                 words_to_partitions(
                     [y_sb[c][:, t, :].bitcast(F32), z_sb[c][:, t, :].bitcast(F32), u_words[:, 0:P], u_words[:, P:2 * P]],
-                    grouped[:].bitcast(F32)[:, :, t * P:(t + 1) * P, :],
+                    f_grouped[c][:].bitcast(F32)[:, :, t * P:(t + 1) * P, :],
                     nc.scalar.copy,
                 )
-            f_codes[c] = work.tile([P, FEAT_PASSES, CHUNK], U32, name="f_codes", tag="f_codes", align_bytes=64, bufs=3)
-            f_scales[c] = work.tile([P, FEAT_PASSES, CHUNK], U8, name="f_scales", tag="f_scales", align_bytes=64, bufs=3)
+
+        def quantise_features(c):
+            f_codes[c] = work.tile([P, FEAT_PASSES, CHUNK], U32, name="f_codes", tag="f_codes", align_bytes=64)
+            f_scales[c] = work.tile([P, FEAT_PASSES, CHUNK], U8, name="f_scales", tag="f_scales", align_bytes=64)
             nc.vector.quantize_mx(
                 out=f_codes[c][:].rearrange("p g r -> p (g r)").bitcast(FP8X4),
                 scales=f_scales[c][:].rearrange("p g r -> p (g r)"),
-                in_=grouped[:].rearrange("p g r t -> p (g r t)"),
+                in_=f_grouped[c][:].rearrange("p g r t -> p (g r t)"),
             )
 
-        front(0)
+        def hidden_layer(c):
+            h_planes[c] = work.tile([P, HID_TILES, CHUNK], BF16, name="h_planes", tag="h_planes")
+            for j in range(HID_TILES):
+                acc = ring_bank([P, CHUNK], F32)
+                for g in range(FEAT_PASSES):
+                    nc.tensor.matmul_mx(
+                        out=acc[:],
+                        lhsT=w1_codes[:, j, g, :].bitcast(FP8X4),
+                        lhsT_scale=w1_scales[:, j, g, :],
+                        rhs=f_codes[c][:, g, :].bitcast(FP8X4),
+                        rhs_scale=f_scales[c][:, g, :],
+                        start=(g == 0),
+                        stop=(g == FEAT_PASSES - 1),
+                    )
+                nc.scalar.activation(out=h_planes[c][:, j, :], in_=acc[:], func=ACT.Tanh, bias=b1_col[:, j:j + 1], scale=1.0)
+
+        def drive_product(c):
+            bu[c] = []
+            for s in range(CHUNK_TILES // PAIR):
+                bank = psum.tile([P, PAIR, MODES], F32, name="bu", tag="bu", bufs=CHUNK_TILES // PAIR)
+                for i in range(PAIR):
+                    cols = slice((s * PAIR + i) * P, (s * PAIR + i + 1) * P)
+                    nc.tensor.matmul_mx(
+                        out=bank[:, i, :],
+                        lhsT=f_codes[c][:, 1, cols].bitcast(FP8X4),
+                        lhsT_scale=f_scales[c][:, 1, cols],
+                        rhs=bt_codes[:].bitcast(FP8X4),
+                        rhs_scale=bt_scales[:],
+                        start=True,
+                        stop=True,
+                    )
+                bu[c].append(bank)
+
+        def regroup_hidden(c):
+            h_grouped[c] = work.tile([P, CHUNK, PACK], BF16, name="h_grouped", tag="h_grouped", align_bytes=64)
+            nc.vector.tensor_copy(
+                out=h_grouped[c][:].rearrange("p (c i) j -> p c j i", i=4),
+                in_=h_planes[c][:].rearrange("p j (c i) -> p c j i", i=4),
+            )
+
+        def quantise_hidden(c):
+            h_codes[c] = work.tile([P, CHUNK], U32, name="h_codes", tag="h_codes", align_bytes=64)
+            h_scales[c] = work.tile([P, CHUNK], U8, name="h_scales", tag="h_scales", align_bytes=64)
+            nc.vector.quantize_mx(
+                out=h_codes[c][:].bitcast(FP8X4),
+                scales=h_scales[c][:],
+                in_=h_grouped[c][:].rearrange("p r j -> p (r j)"),
+            )
+
+        def damping_net(c):
+            th_t[c] = work.tile([P, MODE_TILES, CHUNK], F32, name="th_t", tag="th_t")
+            for m in range(MODE_TILES):
+                cols = slice(m * P, (m + 1) * P)
+                acc = ring_bank([P, CHUNK], F32)
+                nc.tensor.matmul_mx(
+                    out=acc[:],
+                    lhsT=w2_codes[:, cols].bitcast(FP8X4),
+                    lhsT_scale=w2_scales[:, cols],
+                    rhs=h_codes[c][:].bitcast(FP8X4),
+                    rhs_scale=h_scales[c][:],
+                    start=True,
+                    stop=True,
+                )
+                nc.scalar.activation(out=th_t[c][:, m, :], in_=acc[:], func=ACT.Tanh, bias=half_b2_col[:, m:m + 1], scale=0.5)
+
+        def damping_to_states(c):
+            gamma = work.tile([P, CHUNK_TILES, MODES], F32, name="gamma", tag="gamma")
+            for s in range(CHUNK_TILES // PAIR):
+                th = ring_bank([P, PAIR, MODES], F32)
+                for i in range(PAIR):
+                    t = s * PAIR + i
+                    for m in range(MODE_TILES):
+                        nc.tensor.transpose(th[:, i, m * P:(m + 1) * P], th_t[c][:, m, t * P:(t + 1) * P], ident_f32[:])
+                nc.scalar.activation(out=gamma[:, s * PAIR:(s + 1) * PAIR, :], in_=th[:], func=ACT.Identity, bias=1.0, scale=1.0)
+            nc.sync.dma_start(out=gamma_rows[:, chunk_tiles(c), :], in_=gamma[:])
+            keep[c] = work.tile([P, CHUNK_TILES, MODES], F32, name="keep", tag="keep")
+            nc.scalar.activation(out=keep[c][:], in_=gamma[:], func=ACT.Identity, bias=1.0, scale=neg_dt_col[:, 0:1])
+
+        def spring_force(c):
+            spring[c] = work.tile([P, CHUNK_TILES, MODES], F32, name="spring", tag="spring")
+            nc.vector.tensor_tensor(
+                out=spring[c][:], in0=y_sb[c][:],
+                in1=dt_stiff_bc[:].unsqueeze(1).to_broadcast([P, CHUNK_TILES, MODES]), op=ALU.mult,
+            )
+
+        def forced_part(c):
+            forced[c] = work.tile([P, CHUNK_TILES, MODES], F32, name="forced", tag="forced", bufs=3)
+            for s, bank in enumerate(bu[c]):
+                pair = slice(s * PAIR, (s + 1) * PAIR)
+                nc.vector.scalar_tensor_tensor(
+                    out=forced[c][:, pair, :], in0=bank[:], scalar=dt_col[:, 0:1], in1=spring[c][:, pair, :],
+                    op0=ALU.mult, op1=ALU.subtract,
+                )
+
+        def damped_part(c):
+            damped[c] = work.tile([P, CHUNK_TILES, MODES], F32, name="damped", tag="damped")
+            nc.vector.tensor_tensor(out=damped[c][:], in0=keep[c][:], in1=z_sb[c][:], op=ALU.mult)
+
+        def step_z(c):
+            z_next[c] = work.tile([P, CHUNK_TILES, MODES], F32, name="z_next", tag="z_next")
+            nc.vector.tensor_tensor(out=z_next[c][:], in0=damped[c][:], in1=forced[c][:], op=ALU.add)
+            nc.sync.dma_start(out=z_next_rows[:, chunk_tiles(c), :], in_=z_next[c][:])
+
+        def step_y(c):
+            y_next = work.tile([P, CHUNK_TILES, MODES], F32, name="y_next", tag="y_next")
+            nc.vector.scalar_tensor_tensor(
+                out=y_next[:], in0=z_next[c][:], scalar=dt_col[:, 0:1], in1=y_sb[c][:], op0=ALU.mult, op1=ALU.add,
+            )
+            nc.sync.dma_start(out=y_next_rows[:, chunk_tiles(c), :], in_=y_next[:])
+
+        transpose_features(0)
+
+        w1_grouped = consts.tile([P, HID_TILES, FEAT_PASSES, P, PACK], BF16, align_bytes=64)
+        w1_codes = consts.tile([P, HID_TILES, FEAT_PASSES, P], U32, align_bytes=64)
+        w1_scales = consts.tile([P, HID_TILES, FEAT_PASSES, P], U8, align_bytes=64)
+        for j in range(HID_TILES):
+            words = w1_sb[:, j, :].bitcast(F32)
+            words_to_partitions(
+                [words[:, q * P:(q + 1) * P] for q in range(2 * FEAT_PASSES)],
+                w1_grouped[:, j].bitcast(F32),
+                nc.vector.tensor_copy,
+            )
+        quantise_features(0)
+        for j in range(HID_TILES):
+            nc.vector.quantize_mx(
+                out=w1_codes[:, j].rearrange("p g r -> p (g r)").bitcast(FP8X4),
+                scales=w1_scales[:, j].rearrange("p g r -> p (g r)"),
+                in_=w1_grouped[:, j].rearrange("p g r t -> p (g r t)"),
+            )
+
+        bias_bank = ring_bank([P, P], BF16)
+        nc.tensor.transpose(bias_bank[:], bias_rows[:], ident_bf[:])
+        b1_col = consts.tile([P, HID_TILES], F32)
+        nc.vector.tensor_copy(out=b1_col[:], in_=bias_bank[:, 0:HID_TILES])
+        half_b2_col = consts.tile([P, MODE_TILES], F32)
+        nc.vector.tensor_scalar_mul(out=half_b2_col[:], in0=bias_bank[:, HID_TILES:HID_TILES + MODE_TILES], scalar1=0.5)
 
         bt_grouped = consts.tile([P, 1, MODES, PACK], BF16, align_bytes=64)
         bt_codes = consts.tile([P, MODES], U32, align_bytes=64)
@@ -136,34 +270,27 @@ def tile_instrumentedlocmblock_pa_t_kernel(
                 bt_grouped[:].bitcast(F32)[:, :, m * P:(m + 1) * P, :],
                 nc.vector.tensor_copy,
             )
-        nc.vector.quantize_mx(
-            out=bt_codes[:].bitcast(FP8X4),
-            scales=bt_scales[:],
-            in_=bt_grouped[:].rearrange("p g r t -> p (g r t)"),
-        )
 
         w2_grouped = consts.tile([P, MODES, PACK], BF16, align_bytes=64)
         w2_codes = consts.tile([P, MODES], U32, align_bytes=64)
         w2_scales = consts.tile([P, MODES], U8, align_bytes=64)
         for m in range(MODE_TILES):
-            bank = psum.tile([P, HID_TILES, P], BF16, name="bank", tag="tp", bufs=2)
+            bank = ring_bank([P, HID_TILES, P], BF16)
             for j in range(HID_TILES):
                 nc.tensor.transpose(bank[:, j, :], w2_sb[:, m, j * P:(j + 1) * P], ident_bf[:])
             nc.vector.tensor_copy(
                 out=w2_grouped[:, m * P:(m + 1) * P, :], in_=bank[:].rearrange("p j r -> p r j")
             )
         nc.vector.quantize_mx(
+            out=bt_codes[:].bitcast(FP8X4),
+            scales=bt_scales[:],
+            in_=bt_grouped[:].rearrange("p g r t -> p (g r t)"),
+        )
+        nc.vector.quantize_mx(
             out=w2_codes[:].bitcast(FP8X4),
             scales=w2_scales[:],
             in_=w2_grouped[:].rearrange("p r j -> p (r j)"),
         )
-
-        bank = psum.tile([P, P], BF16, name="bank", tag="tp", bufs=2)
-        nc.tensor.transpose(bank[:], bias_rows[:], ident_bf[:])
-        b1_col = consts.tile([P, HID_TILES], F32)
-        nc.vector.tensor_copy(out=b1_col[:], in_=bank[:, 0:HID_TILES])
-        half_b2_col = consts.tile([P, MODE_TILES], F32)
-        nc.vector.tensor_scalar_mul(out=half_b2_col[:], in0=bank[:, HID_TILES:HID_TILES + MODE_TILES], scalar1=0.5)
 
         dt_col = consts.tile([P, 1], F32)
         nc.vector.tensor_copy(out=dt_col[:], in_=dt_bf[:])
@@ -174,104 +301,33 @@ def tile_instrumentedlocmblock_pa_t_kernel(
         dt_stiff_bc = consts.tile([P, MODES], F32)
         nc.vector.tensor_scalar_mul(out=dt_stiff_bc[:], in0=stiff_bc[:], scalar1=dt_col[:, 0:1])
 
-        h_codes, h_scales, forced = {}, {}, {}
+        def live(c):
+            return 0 <= c < N_CHUNKS
 
-        def hidden(c):
-            h_planes = work.tile([P, HID_TILES, CHUNK], BF16, name="h_planes", tag="h_planes")
-            for j in range(HID_TILES):
-                cols = slice(j * P, (j + 1) * P)
-                acc = psum.tile([P, CHUNK], F32, name="h_acc", tag="h", bufs=2)
-                for g in range(FEAT_PASSES):
-                    nc.tensor.matmul_mx(
-                        out=acc[:],
-                        lhsT=w1_codes[:, g, cols].bitcast(FP8X4),
-                        lhsT_scale=w1_scales[:, g, cols],
-                        rhs=f_codes[c][:, g, :].bitcast(FP8X4),
-                        rhs_scale=f_scales[c][:, g, :],
-                        start=(g == 0),
-                        stop=(g == FEAT_PASSES - 1),
-                    )
-                nc.scalar.activation(out=h_planes[:, j, :], in_=acc[:], func=ACT.Tanh, bias=b1_col[:, j:j + 1], scale=1.0)
-            h_grouped = work.tile([P, CHUNK, PACK], BF16, name="h_grouped", tag="h_grouped", align_bytes=64)
-            nc.vector.tensor_copy(
-                out=h_grouped[:].rearrange("p (c i) j -> p c j i", i=4),
-                in_=h_planes[:].rearrange("p j (c i) -> p c j i", i=4),
-            )
-            h_codes[c] = work.tile([P, CHUNK], U32, name="h_codes", tag="h_codes", align_bytes=64)
-            h_scales[c] = work.tile([P, CHUNK], U8, name="h_scales", tag="h_scales", align_bytes=64)
-            nc.vector.quantize_mx(
-                out=h_codes[c][:].bitcast(FP8X4),
-                scales=h_scales[c][:],
-                in_=h_grouped[:].rearrange("p r j -> p (r j)"),
-            )
-
-        def drive(c):
-            spring = work.tile([P, CHUNK_TILES, MODES], F32, name="spring", tag="spring")
-            nc.vector.tensor_tensor(
-                out=spring[:], in0=y_sb[c][:],
-                in1=dt_stiff_bc[:].unsqueeze(1).to_broadcast([P, CHUNK_TILES, MODES]), op=ALU.mult,
-            )
-            forced[c] = work.tile([P, CHUNK_TILES, MODES], F32, name="forced", tag="forced")
-            for s in range(CHUNK_TILES // PAIR):
-                bu = psum.tile([P, PAIR, MODES], F32, name="bu", tag="bu", bufs=1)
-                for i in range(PAIR):
-                    cols = slice((s * PAIR + i) * P, (s * PAIR + i + 1) * P)
-                    nc.tensor.matmul_mx(
-                        out=bu[:, i, :],
-                        lhsT=f_codes[c][:, 1, cols].bitcast(FP8X4),
-                        lhsT_scale=f_scales[c][:, 1, cols],
-                        rhs=bt_codes[:].bitcast(FP8X4),
-                        rhs_scale=bt_scales[:],
-                        start=True,
-                        stop=True,
-                    )
-                pair = slice(s * PAIR, (s + 1) * PAIR)
-                nc.vector.scalar_tensor_tensor(
-                    out=forced[c][:, pair, :], in0=bu[:], scalar=dt_col[:, 0:1], in1=spring[:, pair, :],
-                    op0=ALU.mult, op1=ALU.subtract,
-                )
-
-        def damping_and_step(c):
-            th_t = work.tile([P, MODE_TILES, CHUNK], F32, name="th_t", tag="th_t")
-            for m in range(MODE_TILES):
-                cols = slice(m * P, (m + 1) * P)
-                acc = psum.tile([P, CHUNK], F32, name="g_acc", tag="g", bufs=2)
-                nc.tensor.matmul_mx(
-                    out=acc[:],
-                    lhsT=w2_codes[:, cols].bitcast(FP8X4),
-                    lhsT_scale=w2_scales[:, cols],
-                    rhs=h_codes[c][:].bitcast(FP8X4),
-                    rhs_scale=h_scales[c][:],
-                    start=True,
-                    stop=True,
-                )
-                nc.scalar.activation(out=th_t[:, m, :], in_=acc[:], func=ACT.Tanh, bias=half_b2_col[:, m:m + 1], scale=0.5)
-            gamma = work.tile([P, CHUNK_TILES, MODES], F32, name="gamma", tag="gamma")
-            for s in range(CHUNK_TILES // PAIR):
-                th = psum.tile([P, PAIR, MODES], F32, name="th", tag="th", bufs=1)
-                for i in range(PAIR):
-                    t = s * PAIR + i
-                    for m in range(MODE_TILES):
-                        nc.tensor.transpose(th[:, i, m * P:(m + 1) * P], th_t[:, m, t * P:(t + 1) * P], ident_f32[:])
-                nc.scalar.activation(out=gamma[:, s * PAIR:(s + 1) * PAIR, :], in_=th[:], func=ACT.Identity, bias=1.0, scale=1.0)
-            tiles = slice(c * CHUNK_TILES, (c + 1) * CHUNK_TILES)
-            nc.sync.dma_start(out=gamma_rows[:, tiles, :], in_=gamma[:])
-            keep = work.tile([P, CHUNK_TILES, MODES], F32, name="keep", tag="keep")
-            nc.scalar.activation(out=keep[:], in_=gamma[:], func=ACT.Identity, bias=1.0, scale=neg_dt_col[:, 0:1])
-            damped = work.tile([P, CHUNK_TILES, MODES], F32, name="damped", tag="damped")
-            nc.vector.tensor_tensor(out=damped[:], in0=keep[:], in1=z_sb[c][:], op=ALU.mult)
-            z_next = work.tile([P, CHUNK_TILES, MODES], F32, name="z_next", tag="z_next")
-            nc.vector.tensor_tensor(out=z_next[:], in0=damped[:], in1=forced[c][:], op=ALU.add)
-            nc.sync.dma_start(out=z_next_rows[:, tiles, :], in_=z_next[:])
-            y_next = work.tile([P, CHUNK_TILES, MODES], F32, name="y_next", tag="y_next")
-            nc.vector.scalar_tensor_tensor(
-                out=y_next[:], in0=z_next[:], scalar=dt_col[:, 0:1], in1=y_sb[c][:], op0=ALU.mult, op1=ALU.add,
-            )
-            nc.sync.dma_start(out=y_next_rows[:, tiles, :], in_=y_next[:])
-
-        for c in range(N_CHUNKS):
-            if c + 1 < N_CHUNKS:
-                front(c + 1)
-            hidden(c)
-            drive(c)
-            damping_and_step(c)
+        for i in range(1, N_CHUNKS + 3):
+            first, second, third, fourth = i, i - 1, i - 2, i - 3
+            if live(third):
+                quantise_hidden(third)
+            if live(first):
+                transpose_features(first)
+            if live(third):
+                damping_net(third)
+            if live(fourth):
+                damped_part(fourth)
+            if live(second):
+                spring_force(second)
+            if live(fourth):
+                step_z(fourth)
+            if live(first):
+                quantise_features(first)
+            if live(second):
+                hidden_layer(second)
+                drive_product(second)
+            if live(fourth):
+                step_y(fourth)
+            if live(second):
+                regroup_hidden(second)
+            if live(third):
+                damping_to_states(third)
+            if live(second):
+                forced_part(second)

@@ -203,7 +203,7 @@ def tile_instrumentedlocmblock_pa_t_kernel(
 
         def spring_force(c):
             spring[c] = work.tile([P, CHUNK_TILES, MODES], F32, name="spring", tag="spring")
-            nc.vector.tensor_tensor(
+            nc.gpsimd.tensor_tensor(
                 out=spring[c][:], in0=y_sb[c][:],
                 in1=dt_stiff_bc[:].unsqueeze(1).to_broadcast([P, CHUNK_TILES, MODES]), op=ALU.mult,
             )

@@ -11,18 +11,22 @@ ALU = mybir.AluOpType
 
 P = 128
 PACK = 4
+HALVES = 2
+EVEN_ODD = 2
 BATCH, MODES, DRIVE, HIDDEN = 4096, 256, 512, 512
+FEATS = 2 * MODES + DRIVE
 N_TILES = BATCH // P
 CHUNK_TILES = 4
 CHUNK = CHUNK_TILES * P
 N_CHUNKS = N_TILES // CHUNK_TILES
-FEAT_PASSES = 2
-HID_TILES = HIDDEN // P
-MODE_TILES = MODES // P
+FEAT_PASSES = FEATS // (P * PACK)
+HID_PLANES = HIDDEN // P
 PAIR = 2
-RING_BANKS = 6
+N_PAIRS = CHUNK_TILES // PAIR
+SCALAR_BANKS = 4
+VECTOR_BANKS = 4
 
-FLOPS = 2 * BATCH * (2 * MODES + DRIVE) * HIDDEN + 2 * BATCH * HIDDEN * MODES + 2 * BATCH * DRIVE * MODES
+FLOPS = 2 * BATCH * FEATS * HIDDEN + 2 * BATCH * HIDDEN * MODES + 2 * BATCH * DRIVE * MODES
 
 
 def tile_instrumentedlocmblock_pa_t_kernel(
@@ -41,6 +45,9 @@ def tile_instrumentedlocmblock_pa_t_kernel(
     def chunk_tiles(c):
         return slice(c * CHUNK_TILES, (c + 1) * CHUNK_TILES)
 
+    def tile_cols(t):
+        return slice(t * P, (t + 1) * P)
+
     with tc.tile_pool(name="consts", bufs=1) as consts, \
             tc.tile_pool(name="inputs", bufs=N_CHUNKS) as inputs, \
             tc.tile_pool(name="work", bufs=2) as work, \
@@ -51,10 +58,8 @@ def tile_instrumentedlocmblock_pa_t_kernel(
         nc.vector.memset(warm[:], 0.0)
         nc.scalar.activation(out=warm[:], in_=warm[:], func=ACT.Tanh)
 
-        ident_f32 = consts.tile([P, P], F32)
-        make_identity(nc, ident_f32[:])
-        ident_bf = consts.tile([P, P], BF16)
-        make_identity(nc, ident_bf[:])
+        ident = consts.tile([P, P], F32)
+        make_identity(nc, ident[:])
 
         y_sb, z_sb, u_sb = {}, {}, {}
 
@@ -67,50 +72,71 @@ def tile_instrumentedlocmblock_pa_t_kernel(
             nc.sync.dma_start(out=u_sb[c][:], in_=u_rows[:, chunk_tiles(c), :])
 
         load_chunk(0)
-        w1_sb = consts.tile([P, HID_TILES, 2 * MODES + DRIVE], BF16)
-        w1_rows = dmlp_w1.rearrange("(j p) k -> p j k", p=P)
-        for j in range(HID_TILES):
-            nc.sync.dma_start(out=w1_sb[:, j, :], in_=w1_rows[:, j, :])
-        bias_rows = consts.tile([P, P], BF16)
-        nc.vector.memset(bias_rows[:], 0.0)
-        nc.sync.dma_start(out=bias_rows[0:HID_TILES, :], in_=dmlp_b1.rearrange("(j p) -> j p", p=P))
-        nc.sync.dma_start(
-            out=bias_rows[HID_TILES:HID_TILES + MODE_TILES, :], in_=dmlp_b2.rearrange("(m p) -> m p", p=P)
-        )
-        bt_sb = consts.tile([P, MODE_TILES, DRIVE], BF16)
-        nc.sync.dma_start(out=bt_sb[:], in_=B_tilde.rearrange("(m p) k -> p m k", p=P))
+        w1_sb = consts.tile([P, HALVES, EVEN_ODD, FEATS], BF16)
+        w1_rows = dmlp_w1.rearrange("(h p e) k -> p h e k", h=HALVES, e=EVEN_ODD)
+        for h in range(HALVES):
+            nc.sync.dma_start(out=w1_sb[:, h], in_=w1_rows[:, h])
+        vector_rows = consts.tile([P, EVEN_ODD * P], BF16)
+        nc.vector.memset(vector_rows[:], 0.0)
+        nc.sync.dma_start(out=vector_rows[0:2, :], in_=dmlp_b1.rearrange("(h w) -> h w", h=HALVES))
+        nc.sync.dma_start(out=vector_rows[2:3, :], in_=dmlp_b2.rearrange("(o w) -> o w", o=1))
+        nc.sync.dma_start(out=vector_rows[3:4, :], in_=omega_sq.rearrange("(o w) -> o w", o=1))
+        nc.sync.dma_start(out=vector_rows[4:5, :], in_=alpha_lambda.rearrange("(o w) -> o w", o=1))
+        bt_sb = consts.tile([P, EVEN_ODD, DRIVE], BF16)
+        nc.sync.dma_start(out=bt_sb[:], in_=B_tilde.rearrange("(p e) k -> p e k", e=EVEN_ODD))
         load_chunk(1)
-        w2_sb = consts.tile([P, MODE_TILES, HIDDEN], BF16)
-        nc.sync.dma_start(out=w2_sb[:], in_=dmlp_w2.rearrange("(m p) k -> p m k", p=P))
-        omega_bc = consts.tile([P, MODES], BF16)
-        nc.sync.dma_start(out=omega_bc[:], in_=omega_sq.partition_broadcast(P))
-        alpha_bc = consts.tile([P, MODES], BF16)
-        nc.sync.dma_start(out=alpha_bc[:], in_=alpha_lambda.partition_broadcast(P))
+        w2_sb = consts.tile([P, EVEN_ODD, HIDDEN], BF16)
+        nc.sync.dma_start(out=w2_sb[:], in_=dmlp_w2.rearrange("(p e) k -> p e k", e=EVEN_ODD))
         dt_bf = consts.tile([P, 1], BF16)
         nc.sync.dma_start(out=dt_bf[:], in_=dt.partition_broadcast(P))
         for c in range(2, N_CHUNKS):
             load_chunk(c)
 
-        def ring_bank(shape, dtype):
-            return psum.tile(shape, dtype, name="ring", tag="ring", bufs=RING_BANKS)
+        def scalar_bank(shape):
+            return psum.tile(shape, F32, name="for_scalar", tag="for_scalar", bufs=SCALAR_BANKS)
 
-        def words_to_partitions(word_blocks, grouped_words, copy):
-            bank = ring_bank([P, len(word_blocks), P], F32)
+        def vector_bank(shape):
+            return psum.tile(shape, F32, name="for_vector", tag="for_vector", bufs=VECTOR_BANKS)
+
+        def words_to_partitions(bank, word_blocks, grouped_words, copy):
             for q, block in enumerate(word_blocks):
-                nc.tensor.transpose(bank[:, q, :], block, ident_f32[:])
-            copy(out=grouped_words, in_=bank[:].rearrange("p (g h) r -> p g r h", h=2))
+                nc.tensor.transpose(bank[:, q, :], block, ident[:])
+            copy(out=grouped_words, in_=bank[:].rearrange("p (g h) r -> p g r h", h=HALVES))
+
+        def weight_to_mx(name, rows_sb, blocks, passes):
+            grouped = consts.tile([P, blocks, passes, P, PACK], BF16, name=name + "_grouped", align_bytes=64)
+            codes = consts.tile([P, blocks, passes, P], U32, name=name + "_codes", align_bytes=64)
+            scales = consts.tile([P, blocks, passes, P], U8, name=name + "_scales", align_bytes=64)
+            for b in range(blocks):
+                words = rows_sb[:, b, :].bitcast(F32)
+                words_to_partitions(
+                    vector_bank([P, HALVES * passes, P]),
+                    [words[:, tile_cols(q)] for q in range(HALVES * passes)],
+                    grouped[:, b].bitcast(F32),
+                    nc.vector.tensor_copy,
+                )
+            for b in range(blocks):
+                nc.vector.quantize_mx(
+                    out=codes[:, b].rearrange("p g r -> p (g r)").bitcast(FP8X4),
+                    scales=scales[:, b].rearrange("p g r -> p (g r)"),
+                    in_=grouped[:, b].rearrange("p g r t -> p (g r t)"),
+                )
+            return codes, scales
 
         f_grouped, f_codes, f_scales = {}, {}, {}
         h_planes, h_grouped, h_codes, h_scales = {}, {}, {}, {}
-        bu, spring, forced, th_t, keep, damped, z_next = {}, {}, {}, {}, {}, {}, {}
+        bu_t, accel_t, neg_tanh_t, friction_t, accel, z_next = {}, {}, {}, {}, {}, {}
 
         def transpose_features(c):
-            f_grouped[c] = work.tile([P, FEAT_PASSES, CHUNK, PACK], BF16, name="f_grouped", tag="f_grouped", align_bytes=64)
+            f_grouped[c] = work.tile(
+                [P, FEAT_PASSES, CHUNK, PACK], BF16, name="f_grouped", tag="f_grouped", align_bytes=64, bufs=3
+            )
             for t in range(CHUNK_TILES):
                 u_words = u_sb[c][:, t, :].bitcast(F32)
                 words_to_partitions(
+                    scalar_bank([P, HALVES * FEAT_PASSES, P]),
                     [y_sb[c][:, t, :].bitcast(F32), z_sb[c][:, t, :].bitcast(F32), u_words[:, 0:P], u_words[:, P:2 * P]],
-                    f_grouped[c][:].bitcast(F32)[:, :, t * P:(t + 1) * P, :],
+                    f_grouped[c][:].bitcast(F32)[:, :, tile_cols(t), :],
                     nc.scalar.copy,
                 )
 
@@ -124,9 +150,9 @@ def tile_instrumentedlocmblock_pa_t_kernel(
             )
 
         def hidden_layer(c):
-            h_planes[c] = work.tile([P, HID_TILES, CHUNK], BF16, name="h_planes", tag="h_planes")
-            for j in range(HID_TILES):
-                acc = ring_bank([P, CHUNK], F32)
+            h_planes[c] = work.tile([P, HID_PLANES, CHUNK], BF16, name="h_planes", tag="h_planes")
+            for j in range(HID_PLANES):
+                acc = scalar_bank([P, CHUNK])
                 for g in range(FEAT_PASSES):
                     nc.tensor.matmul_mx(
                         out=acc[:],
@@ -138,23 +164,6 @@ def tile_instrumentedlocmblock_pa_t_kernel(
                         stop=(g == FEAT_PASSES - 1),
                     )
                 nc.scalar.activation(out=h_planes[c][:, j, :], in_=acc[:], func=ACT.Tanh, bias=b1_col[:, j:j + 1], scale=1.0)
-
-        def drive_product(c):
-            bu[c] = []
-            for s in range(CHUNK_TILES // PAIR):
-                bank = psum.tile([P, PAIR, MODES], F32, name="bu", tag="bu", bufs=CHUNK_TILES // PAIR)
-                for i in range(PAIR):
-                    cols = slice((s * PAIR + i) * P, (s * PAIR + i + 1) * P)
-                    nc.tensor.matmul_mx(
-                        out=bank[:, i, :],
-                        lhsT=f_codes[c][:, 1, cols].bitcast(FP8X4),
-                        lhsT_scale=f_scales[c][:, 1, cols],
-                        rhs=bt_codes[:].bitcast(FP8X4),
-                        rhs_scale=bt_scales[:],
-                        start=True,
-                        stop=True,
-                    )
-                bu[c].append(bank)
 
         def regroup_hidden(c):
             h_grouped[c] = work.tile([P, CHUNK, PACK], BF16, name="h_grouped", tag="h_grouped", align_bytes=64)
@@ -172,58 +181,95 @@ def tile_instrumentedlocmblock_pa_t_kernel(
                 in_=h_grouped[c][:].rearrange("p r j -> p (r j)"),
             )
 
+        def drive_product(c):
+            bu_t[c] = []
+            for e in range(EVEN_ODD):
+                bank = vector_bank([P, CHUNK])
+                nc.tensor.matmul_mx(
+                    out=bank[:],
+                    lhsT=bt_codes[:, e, 0, :].bitcast(FP8X4),
+                    lhsT_scale=bt_scales[:, e, 0, :],
+                    rhs=f_codes[c][:, 1, :].bitcast(FP8X4),
+                    rhs_scale=f_scales[c][:, 1, :],
+                    start=True,
+                    stop=True,
+                )
+                bu_t[c].append(bank)
+
+        def undamped_acceleration(c):
+            accel_t[c] = work.tile([P, EVEN_ODD, CHUNK], F32, name="accel_t", tag="accel_t", bufs=3)
+            for e in range(EVEN_ODD):
+                nc.vector.scalar_tensor_tensor(
+                    out=accel_t[c][:, e, :], in0=f_grouped[c][:, 0, :, e], scalar=neg_stiff_col[:, e:e + 1],
+                    in1=bu_t[c][e][:], op0=ALU.mult, op1=ALU.add,
+                )
+
         def damping_net(c):
-            th_t[c] = work.tile([P, MODE_TILES, CHUNK], F32, name="th_t", tag="th_t")
-            for m in range(MODE_TILES):
-                cols = slice(m * P, (m + 1) * P)
-                acc = ring_bank([P, CHUNK], F32)
+            neg_tanh_t[c] = work.tile([P, EVEN_ODD, CHUNK], F32, name="neg_tanh_t", tag="neg_tanh_t")
+            for e in range(EVEN_ODD):
+                acc = scalar_bank([P, CHUNK])
                 nc.tensor.matmul_mx(
                     out=acc[:],
-                    lhsT=w2_codes[:, cols].bitcast(FP8X4),
-                    lhsT_scale=w2_scales[:, cols],
+                    lhsT=w2_codes[:, e, 0, :].bitcast(FP8X4),
+                    lhsT_scale=w2_scales[:, e, 0, :],
                     rhs=h_codes[c][:].bitcast(FP8X4),
                     rhs_scale=h_scales[c][:],
                     start=True,
                     stop=True,
                 )
-                nc.scalar.activation(out=th_t[c][:, m, :], in_=acc[:], func=ACT.Tanh, bias=half_b2_col[:, m:m + 1], scale=0.5)
+                nc.scalar.activation(
+                    out=neg_tanh_t[c][:, e, :], in_=acc[:], func=ACT.Tanh, bias=neg_half_b2_col[:, e:e + 1], scale=-0.5
+                )
 
         def damping_to_states(c):
             gamma = work.tile([P, CHUNK_TILES, MODES], F32, name="gamma", tag="gamma")
-            for s in range(CHUNK_TILES // PAIR):
-                th = ring_bank([P, PAIR, MODES], F32)
+            for s in range(N_PAIRS):
+                bank = scalar_bank([P, PAIR, EVEN_ODD, P])
                 for i in range(PAIR):
-                    t = s * PAIR + i
-                    for m in range(MODE_TILES):
-                        nc.tensor.transpose(th[:, i, m * P:(m + 1) * P], th_t[c][:, m, t * P:(t + 1) * P], ident_f32[:])
-                nc.scalar.activation(out=gamma[:, s * PAIR:(s + 1) * PAIR, :], in_=th[:], func=ACT.Identity, bias=1.0, scale=1.0)
+                    for e in range(EVEN_ODD):
+                        nc.tensor.transpose(bank[:, i, e, :], neg_tanh_t[c][:, e, tile_cols(s * PAIR + i)], ident[:])
+                nc.scalar.activation(
+                    out=gamma[:, s * PAIR:(s + 1) * PAIR, :].rearrange("r i (p e) -> r i p e", e=EVEN_ODD),
+                    in_=bank[:].rearrange("r i e p -> r i p e"),
+                    func=ACT.Identity, bias=1.0, scale=-1.0,
+                )
             nc.sync.dma_start(out=gamma_rows[:, chunk_tiles(c), :], in_=gamma[:])
-            keep[c] = work.tile([P, CHUNK_TILES, MODES], F32, name="keep", tag="keep")
-            nc.scalar.activation(out=keep[c][:], in_=gamma[:], func=ACT.Identity, bias=1.0, scale=neg_dt_col[:, 0:1])
 
-        def spring_force(c):
-            spring[c] = work.tile([P, CHUNK_TILES, MODES], F32, name="spring", tag="spring")
-            nc.gpsimd.tensor_tensor(
-                out=spring[c][:], in0=y_sb[c][:],
-                in1=dt_stiff_bc[:].unsqueeze(1).to_broadcast([P, CHUNK_TILES, MODES]), op=ALU.mult,
+        def friction(c):
+            friction_t[c] = work.tile([P, EVEN_ODD, CHUNK], F32, name="friction_t", tag="friction_t")
+            nc.vector.scalar_tensor_tensor(
+                out=friction_t[c][:], in0=neg_tanh_t[c][:], scalar=-1.0,
+                in1=f_grouped[c][:, 0, :, EVEN_ODD:2 * EVEN_ODD].rearrange("p r e -> p e r"),
+                op0=ALU.add, op1=ALU.mult,
             )
 
-        def forced_part(c):
-            forced[c] = work.tile([P, CHUNK_TILES, MODES], F32, name="forced", tag="forced", bufs=3)
-            for s, bank in enumerate(bu[c]):
-                pair = slice(s * PAIR, (s + 1) * PAIR)
-                nc.vector.scalar_tensor_tensor(
-                    out=forced[c][:, pair, :], in0=bank[:], scalar=dt_col[:, 0:1], in1=spring[c][:, pair, :],
-                    op0=ALU.mult, op1=ALU.subtract,
-                )
-
-        def damped_part(c):
-            damped[c] = work.tile([P, CHUNK_TILES, MODES], F32, name="damped", tag="damped")
-            nc.vector.tensor_tensor(out=damped[c][:], in0=keep[c][:], in1=z_sb[c][:], op=ALU.mult)
+        def acceleration_to_states(c):
+            accel[c] = []
+            for s in range(N_PAIRS):
+                bank = vector_bank([P, PAIR, EVEN_ODD, P])
+                for i in range(PAIR):
+                    for e in range(EVEN_ODD):
+                        cols = tile_cols(s * PAIR + i)
+                        nc.tensor.matmul(
+                            out=bank[:, i, e, :], lhsT=accel_t[c][:, e, cols], rhs=ident[:],
+                            is_transpose=True, start=True, stop=False,
+                        )
+                        nc.tensor.matmul(
+                            out=bank[:, i, e, :], lhsT=friction_t[c][:, e, cols], rhs=ident[:],
+                            is_transpose=True, start=False, stop=True,
+                        )
+                accel[c].append(bank)
 
         def step_z(c):
             z_next[c] = work.tile([P, CHUNK_TILES, MODES], F32, name="z_next", tag="z_next")
-            nc.vector.tensor_tensor(out=z_next[c][:], in0=damped[c][:], in1=forced[c][:], op=ALU.add)
+            for t in range(CHUNK_TILES):
+                nc.vector.scalar_tensor_tensor(
+                    out=z_next[c][:, t, :].rearrange("r (p e) -> r p e", e=EVEN_ODD),
+                    in0=accel[c][t // PAIR][:, t % PAIR].rearrange("r e p -> r p e"),
+                    scalar=dt_col[:, 0:1],
+                    in1=z_sb[c][:, t, :].rearrange("r (p e) -> r p e", e=EVEN_ODD),
+                    op0=ALU.mult, op1=ALU.add,
+                )
             nc.sync.dma_start(out=z_next_rows[:, chunk_tiles(c), :], in_=z_next[c][:])
 
         def step_y(c):
@@ -234,78 +280,32 @@ def tile_instrumentedlocmblock_pa_t_kernel(
             nc.sync.dma_start(out=y_next_rows[:, chunk_tiles(c), :], in_=y_next[:])
 
         transpose_features(0)
-
-        w1_grouped = consts.tile([P, HID_TILES, FEAT_PASSES, P, PACK], BF16, align_bytes=64)
-        w1_codes = consts.tile([P, HID_TILES, FEAT_PASSES, P], U32, align_bytes=64)
-        w1_scales = consts.tile([P, HID_TILES, FEAT_PASSES, P], U8, align_bytes=64)
-        for j in range(HID_TILES):
-            words = w1_sb[:, j, :].bitcast(F32)
-            words_to_partitions(
-                [words[:, q * P:(q + 1) * P] for q in range(2 * FEAT_PASSES)],
-                w1_grouped[:, j].bitcast(F32),
-                nc.vector.tensor_copy,
-            )
+        w1_codes, w1_scales = weight_to_mx("w1", w1_sb[:].rearrange("p h e k -> p (h e) k"), HID_PLANES, FEAT_PASSES)
         quantise_features(0)
-        for j in range(HID_TILES):
-            nc.vector.quantize_mx(
-                out=w1_codes[:, j].rearrange("p g r -> p (g r)").bitcast(FP8X4),
-                scales=w1_scales[:, j].rearrange("p g r -> p (g r)"),
-                in_=w1_grouped[:, j].rearrange("p g r t -> p (g r t)"),
-            )
 
-        bias_bank = ring_bank([P, P], BF16)
-        nc.tensor.transpose(bias_bank[:], bias_rows[:], ident_bf[:])
-        b1_col = consts.tile([P, HID_TILES], F32)
-        nc.vector.tensor_copy(out=b1_col[:], in_=bias_bank[:, 0:HID_TILES])
-        half_b2_col = consts.tile([P, MODE_TILES], F32)
-        nc.vector.tensor_scalar_mul(out=half_b2_col[:], in0=bias_bank[:, HID_TILES:HID_TILES + MODE_TILES], scalar1=0.5)
+        vector_bank_t = vector_bank([P, P])
+        nc.tensor.transpose(vector_bank_t[:], vector_rows[:].bitcast(F32), ident[:])
+        vector_cols = consts.tile([P, 5 * EVEN_ODD], F32)
+        nc.vector.tensor_copy(out=vector_cols[:], in_=vector_bank_t[:, 0:5].bitcast(BF16))
+        b1_col = vector_cols[:, 0:4]
+        neg_half_b2_col = consts.tile([P, EVEN_ODD], F32)
+        nc.vector.tensor_scalar_mul(out=neg_half_b2_col[:], in0=vector_cols[:, 4:6], scalar1=-0.5)
+        neg_stiff_col = consts.tile([P, EVEN_ODD], F32)
+        nc.vector.tensor_tensor(out=neg_stiff_col[:], in0=vector_cols[:, 8:10], in1=vector_cols[:, 6:8], op=ALU.subtract)
 
-        bt_grouped = consts.tile([P, 1, MODES, PACK], BF16, align_bytes=64)
-        bt_codes = consts.tile([P, MODES], U32, align_bytes=64)
-        bt_scales = consts.tile([P, MODES], U8, align_bytes=64)
-        for m in range(MODE_TILES):
-            words = bt_sb[:, m, :].bitcast(F32)
-            words_to_partitions(
-                [words[:, 0:P], words[:, P:2 * P]],
-                bt_grouped[:].bitcast(F32)[:, :, m * P:(m + 1) * P, :],
-                nc.vector.tensor_copy,
-            )
-
-        w2_grouped = consts.tile([P, MODES, PACK], BF16, align_bytes=64)
-        w2_codes = consts.tile([P, MODES], U32, align_bytes=64)
-        w2_scales = consts.tile([P, MODES], U8, align_bytes=64)
-        for m in range(MODE_TILES):
-            bank = ring_bank([P, HID_TILES, P], BF16)
-            for j in range(HID_TILES):
-                nc.tensor.transpose(bank[:, j, :], w2_sb[:, m, j * P:(j + 1) * P], ident_bf[:])
-            nc.vector.tensor_copy(
-                out=w2_grouped[:, m * P:(m + 1) * P, :], in_=bank[:].rearrange("p j r -> p r j")
-            )
-        nc.vector.quantize_mx(
-            out=bt_codes[:].bitcast(FP8X4),
-            scales=bt_scales[:],
-            in_=bt_grouped[:].rearrange("p g r t -> p (g r t)"),
-        )
-        nc.vector.quantize_mx(
-            out=w2_codes[:].bitcast(FP8X4),
-            scales=w2_scales[:],
-            in_=w2_grouped[:].rearrange("p r j -> p (r j)"),
-        )
-
+        bt_codes, bt_scales = weight_to_mx("bt", bt_sb, EVEN_ODD, 1)
+        w2_codes, w2_scales = weight_to_mx("w2", w2_sb, EVEN_ODD, 1)
+        drive_product(0)
         dt_col = consts.tile([P, 1], F32)
         nc.vector.tensor_copy(out=dt_col[:], in_=dt_bf[:])
-        neg_dt_col = consts.tile([P, 1], F32)
-        nc.vector.tensor_scalar_mul(out=neg_dt_col[:], in0=dt_col[:], scalar1=-1.0)
-        stiff_bc = consts.tile([P, MODES], F32)
-        nc.vector.tensor_tensor(out=stiff_bc[:], in0=omega_bc[:], in1=alpha_bc[:], op=ALU.subtract)
-        dt_stiff_bc = consts.tile([P, MODES], F32)
-        nc.vector.tensor_scalar_mul(out=dt_stiff_bc[:], in0=stiff_bc[:], scalar1=dt_col[:, 0:1])
 
         def live(c):
             return 0 <= c < N_CHUNKS
 
         for i in range(1, N_CHUNKS + 3):
             first, second, third, fourth = i, i - 1, i - 2, i - 3
+            if live(second):
+                undamped_acceleration(second)
             if live(third):
                 quantise_hidden(third)
             if live(first):
@@ -313,21 +313,18 @@ def tile_instrumentedlocmblock_pa_t_kernel(
             if live(third):
                 damping_net(third)
             if live(fourth):
-                damped_part(fourth)
-            if live(second):
-                spring_force(second)
-            if live(fourth):
                 step_z(fourth)
             if live(first):
                 quantise_features(first)
             if live(second):
                 hidden_layer(second)
-                drive_product(second)
+            if live(first):
+                drive_product(first)
             if live(fourth):
                 step_y(fourth)
-            if live(second):
-                regroup_hidden(second)
             if live(third):
                 damping_to_states(third)
+                friction(third)
+                acceleration_to_states(third)
             if live(second):
-                forced_part(second)
+                regroup_hidden(second)

@@ -16,13 +16,13 @@ EVEN_ODD = 2
 BATCH, MODES, DRIVE, HIDDEN = 4096, 256, 512, 512
 FEATS = 2 * MODES + DRIVE
 N_TILES = BATCH // P
-CHUNK_TILES = 4
-CHUNK = CHUNK_TILES * P
-N_CHUNKS = N_TILES // CHUNK_TILES
+CHUNK_TILES = (2, 2, 4, 4, 4, 4, 4, 4, 2, 2)
+FIRST_TILE = tuple(sum(CHUNK_TILES[:c]) for c in range(len(CHUNK_TILES)))
+N_CHUNKS = len(CHUNK_TILES)
+MAX_TILES = max(CHUNK_TILES)
 FEAT_PASSES = FEATS // (P * PACK)
 HID_PLANES = HIDDEN // P
 PAIR = 2
-N_PAIRS = CHUNK_TILES // PAIR
 SCALAR_BANKS = 4
 VECTOR_BANKS = 4
 
@@ -43,7 +43,10 @@ def tile_instrumentedlocmblock_pa_t_kernel(
     y_next_rows = out_2.rearrange("(p t) m -> p t m", t=N_TILES)
 
     def chunk_tiles(c):
-        return slice(c * CHUNK_TILES, (c + 1) * CHUNK_TILES)
+        return slice(FIRST_TILE[c], FIRST_TILE[c] + CHUNK_TILES[c])
+
+    def states(c):
+        return CHUNK_TILES[c] * P
 
     def tile_cols(t):
         return slice(t * P, (t + 1) * P)
@@ -64,9 +67,9 @@ def tile_instrumentedlocmblock_pa_t_kernel(
         y_sb, z_sb, u_sb = {}, {}, {}
 
         def load_chunk(c):
-            y_sb[c] = inputs.tile([P, CHUNK_TILES, MODES], BF16, name="y_sb", tag="y")
-            z_sb[c] = inputs.tile([P, CHUNK_TILES, MODES], BF16, name="z_sb", tag="z")
-            u_sb[c] = inputs.tile([P, CHUNK_TILES, DRIVE], BF16, name="u_sb", tag="u")
+            y_sb[c] = inputs.tile([P, CHUNK_TILES[c], MODES], BF16, name="y_sb", tag="y%d" % CHUNK_TILES[c], bufs=CHUNK_TILES.count(CHUNK_TILES[c]))
+            z_sb[c] = inputs.tile([P, CHUNK_TILES[c], MODES], BF16, name="z_sb", tag="z%d" % CHUNK_TILES[c], bufs=CHUNK_TILES.count(CHUNK_TILES[c]))
+            u_sb[c] = inputs.tile([P, CHUNK_TILES[c], DRIVE], BF16, name="u_sb", tag="u%d" % CHUNK_TILES[c], bufs=CHUNK_TILES.count(CHUNK_TILES[c]))
             nc.sync.dma_start(out=y_sb[c][:], in_=y_rows[:, chunk_tiles(c), :])
             nc.sync.dma_start(out=z_sb[c][:], in_=z_rows[:, chunk_tiles(c), :])
             nc.sync.dma_start(out=u_sb[c][:], in_=u_rows[:, chunk_tiles(c), :])
@@ -78,18 +81,17 @@ def tile_instrumentedlocmblock_pa_t_kernel(
             nc.sync.dma_start(out=w1_sb[:, h], in_=w1_rows[:, h])
         vector_rows = consts.tile([P, EVEN_ODD * P], BF16)
         nc.vector.memset(vector_rows[:], 0.0)
-        nc.sync.dma_start(out=vector_rows[0:2, :], in_=dmlp_b1.rearrange("(h w) -> h w", h=HALVES))
-        nc.sync.dma_start(out=vector_rows[2:3, :], in_=dmlp_b2.rearrange("(o w) -> o w", o=1))
-        nc.sync.dma_start(out=vector_rows[3:4, :], in_=omega_sq.rearrange("(o w) -> o w", o=1))
-        nc.sync.dma_start(out=vector_rows[4:5, :], in_=alpha_lambda.rearrange("(o w) -> o w", o=1))
+        nc.gpsimd.dma_start(out=vector_rows[0:2, :], in_=dmlp_b1.rearrange("(h w) -> h w", h=HALVES))
+        nc.gpsimd.dma_start(out=vector_rows[2:3, :], in_=dmlp_b2.rearrange("(o w) -> o w", o=1))
+        nc.gpsimd.dma_start(out=vector_rows[3:4, :], in_=omega_sq.rearrange("(o w) -> o w", o=1))
+        nc.gpsimd.dma_start(out=vector_rows[4:5, :], in_=alpha_lambda.rearrange("(o w) -> o w", o=1))
+        dt_bf = consts.tile([P, 1], BF16)
+        nc.gpsimd.dma_start(out=dt_bf[:], in_=dt.partition_broadcast(P))
         bt_sb = consts.tile([P, EVEN_ODD, DRIVE], BF16)
         nc.sync.dma_start(out=bt_sb[:], in_=B_tilde.rearrange("(p e) k -> p e k", e=EVEN_ODD))
-        load_chunk(1)
         w2_sb = consts.tile([P, EVEN_ODD, HIDDEN], BF16)
         nc.sync.dma_start(out=w2_sb[:], in_=dmlp_w2.rearrange("(p e) k -> p e k", e=EVEN_ODD))
-        dt_bf = consts.tile([P, 1], BF16)
-        nc.sync.dma_start(out=dt_bf[:], in_=dt.partition_broadcast(P))
-        for c in range(2, N_CHUNKS):
+        for c in range(1, N_CHUNKS):
             load_chunk(c)
 
         def scalar_bank(shape):
@@ -98,66 +100,72 @@ def tile_instrumentedlocmblock_pa_t_kernel(
         def vector_bank(shape):
             return psum.tile(shape, F32, name="for_vector", tag="for_vector", bufs=VECTOR_BANKS)
 
-        def words_to_partitions(bank, word_blocks, grouped_words, copy):
+        def words_to_partitions(new_bank, copy, word_blocks, grouped_words):
+            bank = new_bank([P, len(word_blocks), P])
             for q, block in enumerate(word_blocks):
                 nc.tensor.transpose(bank[:, q, :], block, ident[:])
             copy(out=grouped_words, in_=bank[:].rearrange("p (g h) r -> p g r h", h=HALVES))
 
-        def weight_to_mx(name, rows_sb, blocks, passes):
+        def weight_tiles(name, blocks, passes):
             grouped = consts.tile([P, blocks, passes, P, PACK], BF16, name=name + "_grouped", align_bytes=64)
             codes = consts.tile([P, blocks, passes, P], U32, name=name + "_codes", align_bytes=64)
             scales = consts.tile([P, blocks, passes, P], U8, name=name + "_scales", align_bytes=64)
-            for b in range(blocks):
+            return grouped, codes, scales
+
+        def regroup_weight(tiles, rows_sb, blocks, new_bank, copy):
+            word_blocks = []
+            for b in blocks:
                 words = rows_sb[:, b, :].bitcast(F32)
-                words_to_partitions(
-                    vector_bank([P, HALVES * passes, P]),
-                    [words[:, tile_cols(q)] for q in range(HALVES * passes)],
-                    grouped[:, b].bitcast(F32),
-                    nc.vector.tensor_copy,
-                )
-            for b in range(blocks):
-                nc.vector.quantize_mx(
-                    out=codes[:, b].rearrange("p g r -> p (g r)").bitcast(FP8X4),
-                    scales=scales[:, b].rearrange("p g r -> p (g r)"),
-                    in_=grouped[:, b].rearrange("p g r t -> p (g r t)"),
-                )
-            return codes, scales
+                word_blocks += [words[:, tile_cols(q)] for q in range(words.shape[1] // P)]
+            words_to_partitions(
+                new_bank, copy, word_blocks,
+                tiles[0][:, blocks[0]:blocks[-1] + 1].rearrange("p b g r t -> p (b g) r t").bitcast(F32),
+            )
+
+        def quantise_weight(tiles, blocks):
+            grouped, codes, scales = (x[:, blocks[0]:blocks[-1] + 1] for x in tiles)
+            nc.vector.quantize_mx(
+                out=codes.rearrange("p b g r -> p (b g r)").bitcast(FP8X4),
+                scales=scales.rearrange("p b g r -> p (b g r)"),
+                in_=grouped.rearrange("p b g r t -> p (b g r t)"),
+            )
 
         f_grouped, f_codes, f_scales = {}, {}, {}
         h_planes, h_grouped, h_codes, h_scales = {}, {}, {}, {}
         bu_t, accel_t, neg_tanh_t, friction_t, accel, z_next = {}, {}, {}, {}, {}, {}
 
-        def transpose_features(c):
+        def transpose_features(c, turns=((scalar_bank, nc.scalar.copy),)):
             f_grouped[c] = work.tile(
-                [P, FEAT_PASSES, CHUNK, PACK], BF16, name="f_grouped", tag="f_grouped", align_bytes=64, bufs=3
+                [P, FEAT_PASSES, states(c), PACK], BF16, name="f_grouped", tag="f_grouped", align_bytes=64, bufs=4
             )
-            for t in range(CHUNK_TILES):
+            for t in range(CHUNK_TILES[c]):
                 u_words = u_sb[c][:, t, :].bitcast(F32)
+                new_bank, copy = turns[t % len(turns)]
                 words_to_partitions(
-                    scalar_bank([P, HALVES * FEAT_PASSES, P]),
+                    new_bank, copy,
                     [y_sb[c][:, t, :].bitcast(F32), z_sb[c][:, t, :].bitcast(F32), u_words[:, 0:P], u_words[:, P:2 * P]],
                     f_grouped[c][:].bitcast(F32)[:, :, tile_cols(t), :],
-                    nc.scalar.copy,
                 )
 
         def quantise_features(c):
-            f_codes[c] = work.tile([P, FEAT_PASSES, CHUNK], U32, name="f_codes", tag="f_codes", align_bytes=64)
-            f_scales[c] = work.tile([P, FEAT_PASSES, CHUNK], U8, name="f_scales", tag="f_scales", align_bytes=64)
+            f_codes[c] = work.tile([P, FEAT_PASSES, states(c)], U32, name="f_codes", tag="f_codes", align_bytes=64)
+            f_scales[c] = work.tile([P, FEAT_PASSES, states(c)], U8, name="f_scales", tag="f_scales", align_bytes=64)
             nc.vector.quantize_mx(
                 out=f_codes[c][:].rearrange("p g r -> p (g r)").bitcast(FP8X4),
                 scales=f_scales[c][:].rearrange("p g r -> p (g r)"),
                 in_=f_grouped[c][:].rearrange("p g r t -> p (g r t)"),
             )
 
-        def hidden_layer(c):
-            h_planes[c] = work.tile([P, HID_PLANES, CHUNK], BF16, name="h_planes", tag="h_planes")
-            for j in range(HID_PLANES):
-                acc = scalar_bank([P, CHUNK])
+        def hidden_layer(c, planes):
+            if c not in h_planes:
+                h_planes[c] = work.tile([P, HID_PLANES, states(c)], BF16, name="h_planes", tag="h_planes")
+            for j in planes:
+                acc = scalar_bank([P, states(c)])
                 for g in range(FEAT_PASSES):
                     nc.tensor.matmul_mx(
                         out=acc[:],
-                        lhsT=w1_codes[:, j, g, :].bitcast(FP8X4),
-                        lhsT_scale=w1_scales[:, j, g, :],
+                        lhsT=w1[1][:, j, g, :].bitcast(FP8X4),
+                        lhsT_scale=w1[2][:, j, g, :],
                         rhs=f_codes[c][:, g, :].bitcast(FP8X4),
                         rhs_scale=f_scales[c][:, g, :],
                         start=(g == 0),
@@ -166,15 +174,15 @@ def tile_instrumentedlocmblock_pa_t_kernel(
                 nc.scalar.activation(out=h_planes[c][:, j, :], in_=acc[:], func=ACT.Tanh, bias=b1_col[:, j:j + 1], scale=1.0)
 
         def regroup_hidden(c):
-            h_grouped[c] = work.tile([P, CHUNK, PACK], BF16, name="h_grouped", tag="h_grouped", align_bytes=64)
+            h_grouped[c] = work.tile([P, states(c), PACK], BF16, name="h_grouped", tag="h_grouped", align_bytes=64)
             nc.vector.tensor_copy(
                 out=h_grouped[c][:].rearrange("p (c i) j -> p c j i", i=4),
                 in_=h_planes[c][:].rearrange("p j (c i) -> p c j i", i=4),
             )
 
         def quantise_hidden(c):
-            h_codes[c] = work.tile([P, CHUNK], U32, name="h_codes", tag="h_codes", align_bytes=64)
-            h_scales[c] = work.tile([P, CHUNK], U8, name="h_scales", tag="h_scales", align_bytes=64)
+            h_codes[c] = work.tile([P, states(c)], U32, name="h_codes", tag="h_codes", align_bytes=64)
+            h_scales[c] = work.tile([P, states(c)], U8, name="h_scales", tag="h_scales", align_bytes=64)
             nc.vector.quantize_mx(
                 out=h_codes[c][:].bitcast(FP8X4),
                 scales=h_scales[c][:],
@@ -184,11 +192,11 @@ def tile_instrumentedlocmblock_pa_t_kernel(
         def drive_product(c):
             bu_t[c] = []
             for e in range(EVEN_ODD):
-                bank = vector_bank([P, CHUNK])
+                bank = vector_bank([P, states(c)])
                 nc.tensor.matmul_mx(
                     out=bank[:],
-                    lhsT=bt_codes[:, e, 0, :].bitcast(FP8X4),
-                    lhsT_scale=bt_scales[:, e, 0, :],
+                    lhsT=bt[1][:, e, 0, :].bitcast(FP8X4),
+                    lhsT_scale=bt[2][:, e, 0, :],
                     rhs=f_codes[c][:, 1, :].bitcast(FP8X4),
                     rhs_scale=f_scales[c][:, 1, :],
                     start=True,
@@ -197,7 +205,7 @@ def tile_instrumentedlocmblock_pa_t_kernel(
                 bu_t[c].append(bank)
 
         def undamped_acceleration(c):
-            accel_t[c] = work.tile([P, EVEN_ODD, CHUNK], F32, name="accel_t", tag="accel_t", bufs=3)
+            accel_t[c] = work.tile([P, EVEN_ODD, states(c)], F32, name="accel_t", tag="accel_t", bufs=3)
             for e in range(EVEN_ODD):
                 nc.vector.scalar_tensor_tensor(
                     out=accel_t[c][:, e, :], in0=f_grouped[c][:, 0, :, e], scalar=neg_stiff_col[:, e:e + 1],
@@ -205,13 +213,13 @@ def tile_instrumentedlocmblock_pa_t_kernel(
                 )
 
         def damping_net(c):
-            neg_tanh_t[c] = work.tile([P, EVEN_ODD, CHUNK], F32, name="neg_tanh_t", tag="neg_tanh_t")
+            neg_tanh_t[c] = work.tile([P, EVEN_ODD, states(c)], F32, name="neg_tanh_t", tag="neg_tanh_t")
             for e in range(EVEN_ODD):
-                acc = scalar_bank([P, CHUNK])
+                acc = scalar_bank([P, states(c)])
                 nc.tensor.matmul_mx(
                     out=acc[:],
-                    lhsT=w2_codes[:, e, 0, :].bitcast(FP8X4),
-                    lhsT_scale=w2_scales[:, e, 0, :],
+                    lhsT=w2[1][:, e, 0, :].bitcast(FP8X4),
+                    lhsT_scale=w2[2][:, e, 0, :],
                     rhs=h_codes[c][:].bitcast(FP8X4),
                     rhs_scale=h_scales[c][:],
                     start=True,
@@ -222,21 +230,21 @@ def tile_instrumentedlocmblock_pa_t_kernel(
                 )
 
         def damping_to_states(c):
-            gamma = work.tile([P, CHUNK_TILES, MODES], F32, name="gamma", tag="gamma")
-            for s in range(N_PAIRS):
-                bank = scalar_bank([P, PAIR, EVEN_ODD, P])
+            gamma = work.tile([P, CHUNK_TILES[c], MODES], F32, name="gamma", tag="gamma")
+            for s in range(CHUNK_TILES[c] // PAIR):
+                bank = scalar_bank([P, EVEN_ODD, PAIR, P])
                 for i in range(PAIR):
                     for e in range(EVEN_ODD):
-                        nc.tensor.transpose(bank[:, i, e, :], neg_tanh_t[c][:, e, tile_cols(s * PAIR + i)], ident[:])
+                        nc.tensor.transpose(bank[:, e, i, :], neg_tanh_t[c][:, e, tile_cols(s * PAIR + i)], ident[:])
                 nc.scalar.activation(
-                    out=gamma[:, s * PAIR:(s + 1) * PAIR, :].rearrange("r i (p e) -> r i p e", e=EVEN_ODD),
-                    in_=bank[:].rearrange("r i e p -> r i p e"),
+                    out=gamma[:, s * PAIR:(s + 1) * PAIR, :].rearrange("r i (p e) -> r (i p) e", e=EVEN_ODD),
+                    in_=bank[:].rearrange("r e i p -> r (i p) e"),
                     func=ACT.Identity, bias=1.0, scale=-1.0,
                 )
             nc.sync.dma_start(out=gamma_rows[:, chunk_tiles(c), :], in_=gamma[:])
 
         def friction(c):
-            friction_t[c] = work.tile([P, EVEN_ODD, CHUNK], F32, name="friction_t", tag="friction_t")
+            friction_t[c] = work.tile([P, EVEN_ODD, states(c)], F32, name="friction_t", tag="friction_t")
             nc.vector.scalar_tensor_tensor(
                 out=friction_t[c][:], in0=neg_tanh_t[c][:], scalar=-1.0,
                 in1=f_grouped[c][:, 0, :, EVEN_ODD:2 * EVEN_ODD].rearrange("p r e -> p e r"),
@@ -245,86 +253,101 @@ def tile_instrumentedlocmblock_pa_t_kernel(
 
         def acceleration_to_states(c):
             accel[c] = []
-            for s in range(N_PAIRS):
-                bank = vector_bank([P, PAIR, EVEN_ODD, P])
+            for s in range(CHUNK_TILES[c] // PAIR):
+                bank = vector_bank([P, EVEN_ODD, PAIR, P])
                 for i in range(PAIR):
                     for e in range(EVEN_ODD):
                         cols = tile_cols(s * PAIR + i)
                         nc.tensor.matmul(
-                            out=bank[:, i, e, :], lhsT=accel_t[c][:, e, cols], rhs=ident[:],
+                            out=bank[:, e, i, :], lhsT=accel_t[c][:, e, cols], rhs=ident[:],
                             is_transpose=True, start=True, stop=False,
                         )
                         nc.tensor.matmul(
-                            out=bank[:, i, e, :], lhsT=friction_t[c][:, e, cols], rhs=ident[:],
+                            out=bank[:, e, i, :], lhsT=friction_t[c][:, e, cols], rhs=ident[:],
                             is_transpose=True, start=False, stop=True,
                         )
                 accel[c].append(bank)
 
         def step_z(c):
-            z_next[c] = work.tile([P, CHUNK_TILES, MODES], F32, name="z_next", tag="z_next")
-            for t in range(CHUNK_TILES):
+            z_next[c] = work.tile([P, CHUNK_TILES[c], MODES], F32, name="z_next", tag="z_next")
+            for s in range(CHUNK_TILES[c] // PAIR):
+                tiles = slice(s * PAIR, (s + 1) * PAIR)
                 nc.vector.scalar_tensor_tensor(
-                    out=z_next[c][:, t, :].rearrange("r (p e) -> r p e", e=EVEN_ODD),
-                    in0=accel[c][t // PAIR][:, t % PAIR].rearrange("r e p -> r p e"),
+                    out=z_next[c][:, tiles, :].rearrange("r i (p e) -> r (i p) e", e=EVEN_ODD),
+                    in0=accel[c][s][:].rearrange("r e i p -> r (i p) e"),
                     scalar=dt_col[:, 0:1],
-                    in1=z_sb[c][:, t, :].rearrange("r (p e) -> r p e", e=EVEN_ODD),
+                    in1=z_sb[c][:, tiles, :].rearrange("r i (p e) -> r (i p) e", e=EVEN_ODD),
                     op0=ALU.mult, op1=ALU.add,
                 )
             nc.sync.dma_start(out=z_next_rows[:, chunk_tiles(c), :], in_=z_next[c][:])
 
         def step_y(c):
-            y_next = work.tile([P, CHUNK_TILES, MODES], F32, name="y_next", tag="y_next")
+            y_next = work.tile([P, CHUNK_TILES[c], MODES], F32, name="y_next", tag="y_next")
             nc.vector.scalar_tensor_tensor(
                 out=y_next[:], in0=z_next[c][:], scalar=dt_col[:, 0:1], in1=y_sb[c][:], op0=ALU.mult, op1=ALU.add,
             )
             nc.sync.dma_start(out=y_next_rows[:, chunk_tiles(c), :], in_=y_next[:])
 
+        on_scalar, on_vector = (scalar_bank, nc.scalar.copy), (vector_bank, nc.vector.tensor_copy)
+        w1 = weight_tiles("w1", HID_PLANES, FEAT_PASSES)
+        bt = weight_tiles("bt", EVEN_ODD, 1)
+        w2 = weight_tiles("w2", EVEN_ODD, 1)
+        w1_sb_blocks = w1_sb[:].rearrange("p h e k -> p (h e) k")
         transpose_features(0)
-        w1_codes, w1_scales = weight_to_mx("w1", w1_sb[:].rearrange("p h e k -> p (h e) k"), HID_PLANES, FEAT_PASSES)
         quantise_features(0)
-
+        for b in range(HID_PLANES):
+            regroup_weight(w1, w1_sb_blocks, [b], *(on_vector, on_scalar)[b % 2])
         vector_bank_t = vector_bank([P, P])
         nc.tensor.transpose(vector_bank_t[:], vector_rows[:].bitcast(F32), ident[:])
         vector_cols = consts.tile([P, 5 * EVEN_ODD], F32)
         nc.vector.tensor_copy(out=vector_cols[:], in_=vector_bank_t[:, 0:5].bitcast(BF16))
         b1_col = vector_cols[:, 0:4]
+        for b in range(HID_PLANES):
+            quantise_weight(w1, [b])
         neg_half_b2_col = consts.tile([P, EVEN_ODD], F32)
         nc.vector.tensor_scalar_mul(out=neg_half_b2_col[:], in0=vector_cols[:, 4:6], scalar1=-0.5)
         neg_stiff_col = consts.tile([P, EVEN_ODD], F32)
         nc.vector.tensor_tensor(out=neg_stiff_col[:], in0=vector_cols[:, 8:10], in1=vector_cols[:, 6:8], op=ALU.subtract)
-
-        bt_codes, bt_scales = weight_to_mx("bt", bt_sb, EVEN_ODD, 1)
-        w2_codes, w2_scales = weight_to_mx("w2", w2_sb, EVEN_ODD, 1)
-        drive_product(0)
         dt_col = consts.tile([P, 1], F32)
         nc.vector.tensor_copy(out=dt_col[:], in_=dt_bf[:])
 
-        def live(c):
-            return 0 <= c < N_CHUNKS
-
+        regroup_weight(bt, bt_sb, [0, 1], *on_vector)
+        regroup_weight(w2, w2_sb, [0, 1], *on_vector)
+        transpose_features(1)
+        hidden_layer(0, range(HID_PLANES))
+        quantise_weight(bt, [0, 1])
+        quantise_features(1)
+        drive_product(0)
+        quantise_weight(w2, [0, 1])
+        undamped_acceleration(0)
         for i in range(1, N_CHUNKS + 3):
-            first, second, third, fourth = i, i - 1, i - 2, i - 3
-            if live(second):
-                undamped_acceleration(second)
-            if live(third):
-                quantise_hidden(third)
-            if live(first):
-                transpose_features(first)
-            if live(third):
-                damping_net(third)
-            if live(fourth):
-                step_z(fourth)
-            if live(first):
-                quantise_features(first)
-            if live(second):
-                hidden_layer(second)
-            if live(first):
-                drive_product(first)
-            if live(fourth):
-                step_y(fourth)
-            if live(third):
-                damping_to_states(third)
-                friction(third)
-                acceleration_to_states(third)
-            if live(second):
-                regroup_hidden(second)
+            if 2 <= i - 0 < N_CHUNKS:
+                transpose_features(i - 0)
+            if 1 <= i - 1 < N_CHUNKS:
+                undamped_acceleration(i - 1)
+            if 0 <= i - 2 < N_CHUNKS:
+                regroup_hidden(i - 2)
+            if 1 <= i - 1 < N_CHUNKS:
+                hidden_layer(i - 1, (0, 1))
+            if 0 <= i - 2 < N_CHUNKS:
+                quantise_hidden(i - 2)
+            if 0 <= i - 3 < N_CHUNKS:
+                acceleration_to_states(i - 3)
+            if 2 <= i - 0 < N_CHUNKS:
+                quantise_features(i - 0)
+            if 0 <= i - 2 < N_CHUNKS:
+                damping_net(i - 2)
+            if 1 <= i - 1 < N_CHUNKS:
+                hidden_layer(i - 1, (2,))
+            if 0 <= i - 3 < N_CHUNKS:
+                step_z(i - 3)
+            if 0 <= i - 3 < N_CHUNKS:
+                damping_to_states(i - 3)
+            if 0 <= i - 3 < N_CHUNKS:
+                step_y(i - 3)
+            if 1 <= i - 1 < N_CHUNKS:
+                hidden_layer(i - 1, (3,))
+            if 1 <= i - 0 < N_CHUNKS:
+                drive_product(i - 0)
+            if 0 <= i - 2 < N_CHUNKS:
+                friction(i - 2)

@@ -81,17 +81,19 @@ def tile_instrumentedlocmblock_pa_t_kernel(
             nc.sync.dma_start(out=w1_sb[:, h], in_=w1_rows[:, h])
         vector_rows = consts.tile([P, EVEN_ODD * P], BF16)
         nc.vector.memset(vector_rows[:], 0.0)
-        nc.gpsimd.dma_start(out=vector_rows[0:2, :], in_=dmlp_b1.rearrange("(h w) -> h w", h=HALVES))
-        nc.gpsimd.dma_start(out=vector_rows[2:3, :], in_=dmlp_b2.rearrange("(o w) -> o w", o=1))
-        nc.gpsimd.dma_start(out=vector_rows[3:4, :], in_=omega_sq.rearrange("(o w) -> o w", o=1))
-        nc.gpsimd.dma_start(out=vector_rows[4:5, :], in_=alpha_lambda.rearrange("(o w) -> o w", o=1))
-        dt_bf = consts.tile([P, 1], BF16)
-        nc.gpsimd.dma_start(out=dt_bf[:], in_=dt.partition_broadcast(P))
+        nc.sync.dma_start(out=vector_rows[0:2, :], in_=dmlp_b1.rearrange("(h w) -> h w", h=HALVES))
+        nc.sync.dma_start(out=vector_rows[2:3, :], in_=dmlp_b2.rearrange("(o w) -> o w", o=1))
+        nc.sync.dma_start(out=vector_rows[3:4, :], in_=omega_sq.rearrange("(o w) -> o w", o=1))
+        nc.sync.dma_start(out=vector_rows[4:5, :], in_=alpha_lambda.rearrange("(o w) -> o w", o=1))
         bt_sb = consts.tile([P, EVEN_ODD, DRIVE], BF16)
         nc.sync.dma_start(out=bt_sb[:], in_=B_tilde.rearrange("(p e) k -> p e k", e=EVEN_ODD))
         w2_sb = consts.tile([P, EVEN_ODD, HIDDEN], BF16)
         nc.sync.dma_start(out=w2_sb[:], in_=dmlp_w2.rearrange("(p e) k -> p e k", e=EVEN_ODD))
-        for c in range(1, N_CHUNKS):
+        for c in range(1, 4):
+            load_chunk(c)
+        dt_bf = consts.tile([P, 1], BF16)
+        nc.sync.dma_start(out=dt_bf[:], in_=dt.partition_broadcast(P))
+        for c in range(4, N_CHUNKS):
             load_chunk(c)
 
         def scalar_bank(shape):
@@ -308,8 +310,6 @@ def tile_instrumentedlocmblock_pa_t_kernel(
         nc.vector.tensor_scalar_mul(out=neg_half_b2_col[:], in0=vector_cols[:, 4:6], scalar1=-0.5)
         neg_stiff_col = consts.tile([P, EVEN_ODD], F32)
         nc.vector.tensor_tensor(out=neg_stiff_col[:], in0=vector_cols[:, 8:10], in1=vector_cols[:, 6:8], op=ALU.subtract)
-        dt_col = consts.tile([P, 1], F32)
-        nc.vector.tensor_copy(out=dt_col[:], in_=dt_bf[:])
 
         regroup_weight(bt, bt_sb, [0, 1], *on_vector)
         regroup_weight(w2, w2_sb, [0, 1], *on_vector)
@@ -320,34 +320,37 @@ def tile_instrumentedlocmblock_pa_t_kernel(
         drive_product(0)
         quantise_weight(w2, [0, 1])
         undamped_acceleration(0)
+        dt_col = consts.tile([P, 1], F32)
         for i in range(1, N_CHUNKS + 3):
             if 2 <= i - 0 < N_CHUNKS:
                 transpose_features(i - 0)
-            if 1 <= i - 1 < N_CHUNKS:
-                undamped_acceleration(i - 1)
             if 0 <= i - 2 < N_CHUNKS:
                 regroup_hidden(i - 2)
+            if 1 <= i - 1 < N_CHUNKS:
+                undamped_acceleration(i - 1)
             if 1 <= i - 1 < N_CHUNKS:
                 hidden_layer(i - 1, (0, 1))
             if 0 <= i - 2 < N_CHUNKS:
                 quantise_hidden(i - 2)
             if 0 <= i - 3 < N_CHUNKS:
                 acceleration_to_states(i - 3)
+            if 0 <= i - 3 < N_CHUNKS:
+                if i == 3:
+                    nc.vector.tensor_copy(out=dt_col[:], in_=dt_bf[:])
+                step_z(i - 3)
             if 2 <= i - 0 < N_CHUNKS:
                 quantise_features(i - 0)
             if 0 <= i - 2 < N_CHUNKS:
                 damping_net(i - 2)
             if 1 <= i - 1 < N_CHUNKS:
                 hidden_layer(i - 1, (2,))
-            if 0 <= i - 3 < N_CHUNKS:
-                step_z(i - 3)
+            if 1 <= i - 1 < N_CHUNKS:
+                hidden_layer(i - 1, (3,))
             if 0 <= i - 3 < N_CHUNKS:
                 damping_to_states(i - 3)
             if 0 <= i - 3 < N_CHUNKS:
                 step_y(i - 3)
-            if 1 <= i - 1 < N_CHUNKS:
-                hidden_layer(i - 1, (3,))
-            if 1 <= i - 0 < N_CHUNKS:
-                drive_product(i - 0)
             if 0 <= i - 2 < N_CHUNKS:
                 friction(i - 2)
+            if 1 <= i - 0 < N_CHUNKS:
+                drive_product(i - 0)

@@ -253,9 +253,9 @@ def tile_instrumentedlocmblock_pa_t_kernel(
                 op0=ALU.add, op1=ALU.mult,
             )
 
-        def acceleration_to_states(c):
-            accel[c] = []
-            for s in range(CHUNK_TILES[c] // PAIR):
+        def acceleration_to_states(c, pairs):
+            accel.setdefault(c, [])
+            for s in pairs:
                 bank = vector_bank([P, EVEN_ODD, PAIR, P])
                 for i in range(PAIR):
                     for e in range(EVEN_ODD):
@@ -270,9 +270,10 @@ def tile_instrumentedlocmblock_pa_t_kernel(
                         )
                 accel[c].append(bank)
 
-        def step_z(c):
-            z_next[c] = work.tile([P, CHUNK_TILES[c], MODES], F32, name="z_next", tag="z_next")
-            for s in range(CHUNK_TILES[c] // PAIR):
+        def step_z(c, pairs):
+            if c not in z_next:
+                z_next[c] = work.tile([P, CHUNK_TILES[c], MODES], F32, name="z_next", tag="z_next")
+            for s in pairs:
                 tiles = slice(s * PAIR, (s + 1) * PAIR)
                 nc.vector.scalar_tensor_tensor(
                     out=z_next[c][:, tiles, :].rearrange("r i (p e) -> r (i p) e", e=EVEN_ODD),
@@ -281,7 +282,8 @@ def tile_instrumentedlocmblock_pa_t_kernel(
                     in1=z_sb[c][:, tiles, :].rearrange("r i (p e) -> r (i p) e", e=EVEN_ODD),
                     op0=ALU.mult, op1=ALU.add,
                 )
-            nc.sync.dma_start(out=z_next_rows[:, chunk_tiles(c), :], in_=z_next[c][:])
+            if CHUNK_TILES[c] // PAIR - 1 in pairs:
+                nc.sync.dma_start(out=z_next_rows[:, chunk_tiles(c), :], in_=z_next[c][:])
 
         def step_y(c):
             y_next = work.tile([P, CHUNK_TILES[c], MODES], F32, name="y_next", tag="y_next")
@@ -322,35 +324,50 @@ def tile_instrumentedlocmblock_pa_t_kernel(
         undamped_acceleration(0)
         dt_col = consts.tile([P, 1], F32)
         for i in range(1, N_CHUNKS + 3):
-            if 2 <= i - 0 < N_CHUNKS:
-                transpose_features(i - 0)
-            if 0 <= i - 2 < N_CHUNKS:
-                regroup_hidden(i - 2)
-            if 1 <= i - 1 < N_CHUNKS:
-                undamped_acceleration(i - 1)
-            if 1 <= i - 1 < N_CHUNKS:
-                hidden_layer(i - 1, (0, 1))
-            if 0 <= i - 2 < N_CHUNKS:
-                quantise_hidden(i - 2)
-            if 0 <= i - 3 < N_CHUNKS:
-                acceleration_to_states(i - 3)
-            if 0 <= i - 3 < N_CHUNKS:
-                if i == 3:
+            c = i - 0
+            if 2 <= c < N_CHUNKS:
+                transpose_features(c)
+            c = i - 3
+            if 0 <= c < N_CHUNKS:
+                acceleration_to_states(c, range(CHUNK_TILES[c] // PAIR))
+            c = i - 2
+            if 0 <= c < N_CHUNKS:
+                regroup_hidden(c)
+            c = i - 1
+            if 1 <= c < N_CHUNKS:
+                undamped_acceleration(c)
+            c = i - 1
+            if 1 <= c < N_CHUNKS:
+                hidden_layer(c, (0, 1))
+            c = i - 2
+            if 0 <= c < N_CHUNKS:
+                quantise_hidden(c)
+            c = i - 3
+            if 0 <= c < N_CHUNKS:
+                if c == 0:
                     nc.vector.tensor_copy(out=dt_col[:], in_=dt_bf[:])
-                step_z(i - 3)
-            if 2 <= i - 0 < N_CHUNKS:
-                quantise_features(i - 0)
-            if 0 <= i - 2 < N_CHUNKS:
-                damping_net(i - 2)
-            if 1 <= i - 1 < N_CHUNKS:
-                hidden_layer(i - 1, (2,))
-            if 1 <= i - 1 < N_CHUNKS:
-                hidden_layer(i - 1, (3,))
-            if 0 <= i - 3 < N_CHUNKS:
-                damping_to_states(i - 3)
-            if 0 <= i - 3 < N_CHUNKS:
-                step_y(i - 3)
-            if 0 <= i - 2 < N_CHUNKS:
-                friction(i - 2)
-            if 1 <= i - 0 < N_CHUNKS:
-                drive_product(i - 0)
+                step_z(c, range(CHUNK_TILES[c] // PAIR))
+            c = i - 0
+            if 2 <= c < N_CHUNKS:
+                quantise_features(c)
+            c = i - 2
+            if 0 <= c < N_CHUNKS:
+                damping_net(c)
+            c = i - 1
+            if 1 <= c < N_CHUNKS:
+                hidden_layer(c, (2,))
+            c = i - 1
+            if 1 <= c < N_CHUNKS:
+                hidden_layer(c, (3,))
+            c = i - 3
+            if 0 <= c < N_CHUNKS:
+                step_y(c)
+            c = i - 2
+            if 0 <= c < N_CHUNKS:
+                friction(c)
+            c = i - 0
+            if 1 <= c < N_CHUNKS:
+                drive_product(c)
+            c = i - 3
+            if 0 <= c < N_CHUNKS:
+                damping_to_states(c)

@@ -79,21 +79,25 @@ def tile_instrumentedlocmblock_pa_t_kernel(
         w1_rows = dmlp_w1.rearrange("(h p e) k -> p h e k", h=HALVES, e=EVEN_ODD)
         for h in range(HALVES):
             nc.sync.dma_start(out=w1_sb[:, h], in_=w1_rows[:, h])
-        vector_rows = consts.tile([P, EVEN_ODD * P], BF16)
-        nc.vector.memset(vector_rows[:], 0.0)
-        nc.sync.dma_start(out=vector_rows[0:2, :], in_=dmlp_b1.rearrange("(h w) -> h w", h=HALVES))
-        nc.sync.dma_start(out=vector_rows[2:3, :], in_=dmlp_b2.rearrange("(o w) -> o w", o=1))
-        nc.sync.dma_start(out=vector_rows[3:4, :], in_=omega_sq.rearrange("(o w) -> o w", o=1))
-        nc.sync.dma_start(out=vector_rows[4:5, :], in_=alpha_lambda.rearrange("(o w) -> o w", o=1))
+        b1_rows = consts.tile([P, EVEN_ODD * P], BF16)
+        nc.vector.memset(b1_rows[:], 0.0)
+        mode_rows = consts.tile([P, EVEN_ODD * P], BF16)
+        nc.vector.memset(mode_rows[:], 0.0)
+        dt_row = consts.tile([P, 2], BF16)
+        nc.vector.memset(dt_row[:], 0.0)
+        ones = consts.tile([P, 2], BF16)
+        nc.vector.memset(ones[:], 1.0)
         bt_sb = consts.tile([P, EVEN_ODD, DRIVE], BF16)
-        nc.sync.dma_start(out=bt_sb[:], in_=B_tilde.rearrange("(p e) k -> p e k", e=EVEN_ODD))
         w2_sb = consts.tile([P, EVEN_ODD, HIDDEN], BF16)
+        nc.sync.dma_start(out=b1_rows[0:2, :], in_=dmlp_b1.rearrange("(h w) -> h w", h=HALVES))
+        load_chunk(1)
+        nc.sync.dma_start(out=bt_sb[:], in_=B_tilde.rearrange("(p e) k -> p e k", e=EVEN_ODD))
         nc.sync.dma_start(out=w2_sb[:], in_=dmlp_w2.rearrange("(p e) k -> p e k", e=EVEN_ODD))
-        for c in range(1, 4):
-            load_chunk(c)
-        dt_bf = consts.tile([P, 1], BF16)
-        nc.sync.dma_start(out=dt_bf[:], in_=dt.partition_broadcast(P))
-        for c in range(4, N_CHUNKS):
+        load_chunk(2)
+        for row, vector in enumerate((dmlp_b2, omega_sq, alpha_lambda)):
+            nc.sync.dma_start(out=mode_rows[row:row + 1, :], in_=vector.rearrange("(o w) -> o w", o=1))
+        nc.sync.dma_start(out=dt_row[0:1, 0:1], in_=dt.rearrange("(o w) -> o w", o=1))
+        for c in range(3, N_CHUNKS):
             load_chunk(c)
 
         def scalar_bank(shape):
@@ -301,32 +305,36 @@ def tile_instrumentedlocmblock_pa_t_kernel(
         quantise_features(0)
         for b in range(HID_PLANES):
             regroup_weight(w1, w1_sb_blocks, [b], *(on_vector, on_scalar)[b % 2])
-        vector_bank_t = vector_bank([P, P])
-        nc.tensor.transpose(vector_bank_t[:], vector_rows[:].bitcast(F32), ident[:])
-        vector_cols = consts.tile([P, 5 * EVEN_ODD], F32)
-        nc.vector.tensor_copy(out=vector_cols[:], in_=vector_bank_t[:, 0:5].bitcast(BF16))
-        b1_col = vector_cols[:, 0:4]
+        b1_bank = vector_bank([P, P])
+        nc.tensor.transpose(b1_bank[:], b1_rows[:].bitcast(F32), ident[:])
+        b1_col = consts.tile([P, HID_PLANES], F32)
+        nc.vector.tensor_copy(out=b1_col[:], in_=b1_bank[:, 0:2].bitcast(BF16))
         for b in range(HID_PLANES):
             quantise_weight(w1, [b])
-        neg_half_b2_col = consts.tile([P, EVEN_ODD], F32)
-        nc.vector.tensor_scalar_mul(out=neg_half_b2_col[:], in0=vector_cols[:, 4:6], scalar1=-0.5)
-        neg_stiff_col = consts.tile([P, EVEN_ODD], F32)
-        nc.vector.tensor_tensor(out=neg_stiff_col[:], in0=vector_cols[:, 8:10], in1=vector_cols[:, 6:8], op=ALU.subtract)
-
+        transpose_features(1)
+        quantise_features(1)
+        hidden_layer(0, range(HID_PLANES))
         regroup_weight(bt, bt_sb, [0, 1], *on_vector)
         regroup_weight(w2, w2_sb, [0, 1], *on_vector)
-        transpose_features(1)
-        hidden_layer(0, range(HID_PLANES))
         quantise_weight(bt, [0, 1])
-        quantise_features(1)
-        drive_product(0)
         quantise_weight(w2, [0, 1])
-        undamped_acceleration(0)
-        dt_col = consts.tile([P, 1], F32)
-        for i in range(1, N_CHUNKS + 3):
+        for i in range(2, N_CHUNKS + 3):
             c = i - 0
             if 2 <= c < N_CHUNKS:
                 transpose_features(c)
+            if i == 2:
+                mode_bank = vector_bank([P, P])
+                nc.tensor.transpose(mode_bank[:], mode_rows[:].bitcast(F32), ident[:])
+                mode_cols = consts.tile([P, 3 * EVEN_ODD], F32)
+                nc.vector.tensor_copy(out=mode_cols[:], in_=mode_bank[:, 0:3].bitcast(BF16))
+                neg_half_b2_col = consts.tile([P, EVEN_ODD], F32)
+                nc.vector.tensor_scalar_mul(out=neg_half_b2_col[:], in0=mode_cols[:, 0:2], scalar1=-0.5)
+                neg_stiff_col = consts.tile([P, EVEN_ODD], F32)
+                nc.vector.tensor_tensor(out=neg_stiff_col[:], in0=mode_cols[:, 4:6], in1=mode_cols[:, 2:4], op=ALU.subtract)
+                dt_bank = vector_bank([P, 2])
+                nc.tensor.matmul(out=dt_bank[:], lhsT=dt_row[:, 0:1].to_broadcast([P, P]), rhs=ones[:], start=True, stop=True)
+                dt_col = consts.tile([P, 1], F32)
+                nc.vector.tensor_copy(out=dt_col[:], in_=dt_bank[:, 0:1])
             c = i - 3
             if 0 <= c < N_CHUNKS:
                 acceleration_to_states(c, range(CHUNK_TILES[c] // PAIR))
@@ -334,22 +342,26 @@ def tile_instrumentedlocmblock_pa_t_kernel(
             if 0 <= c < N_CHUNKS:
                 regroup_hidden(c)
             c = i - 1
-            if 1 <= c < N_CHUNKS:
+            if 2 <= c < N_CHUNKS:
                 undamped_acceleration(c)
             c = i - 1
             if 1 <= c < N_CHUNKS:
                 hidden_layer(c, (0, 1))
+            if i == 2:
+                drive_product(0)
+                drive_product(1)
             c = i - 2
             if 0 <= c < N_CHUNKS:
                 quantise_hidden(c)
             c = i - 3
             if 0 <= c < N_CHUNKS:
-                if c == 0:
-                    nc.vector.tensor_copy(out=dt_col[:], in_=dt_bf[:])
                 step_z(c, range(CHUNK_TILES[c] // PAIR))
             c = i - 0
             if 2 <= c < N_CHUNKS:
                 quantise_features(c)
+            if i == 2:
+                undamped_acceleration(0)
+                undamped_acceleration(1)
             c = i - 2
             if 0 <= c < N_CHUNKS:
                 damping_net(c)
@@ -366,7 +378,7 @@ def tile_instrumentedlocmblock_pa_t_kernel(
             if 0 <= c < N_CHUNKS:
                 friction(c)
             c = i - 0
-            if 1 <= c < N_CHUNKS:
+            if 2 <= c < N_CHUNKS:
                 drive_product(c)
             c = i - 3
             if 0 <= c < N_CHUNKS:

@@ -24,6 +24,8 @@ FEAT_PASSES = FEATS // (P * PACK)
 HID_PLANES = HIDDEN // P
 PAIR = 2
 SCALAR_BANKS = 4
+CLOCK_COLS = 512
+BANK = 512
 VECTOR_BANKS = 4
 
 FLOPS = 2 * BATCH * FEATS * HIDDEN + 2 * BATCH * HIDDEN * MODES + 2 * BATCH * DRIVE * MODES
@@ -47,6 +49,9 @@ def tile_instrumentedlocmblock_pa_t_kernel(
 
     def states(c):
         return CHUNK_TILES[c] * P
+
+    def pairs(c):
+        return [range(t, min(t + PAIR, CHUNK_TILES[c])) for t in range(0, CHUNK_TILES[c], PAIR)]
 
     def tile_cols(t):
         return slice(t * P, (t + 1) * P)
@@ -197,10 +202,12 @@ def tile_instrumentedlocmblock_pa_t_kernel(
 
         def drive_product(c):
             bu_t[c] = []
+            share = min(EVEN_ODD, BANK // states(c))
             for e in range(EVEN_ODD):
-                bank = vector_bank([P, states(c)])
+                if e % share == 0:
+                    bank = vector_bank([P, share, states(c)])
                 nc.tensor.matmul_mx(
-                    out=bank[:],
+                    out=bank[:, e % share, :],
                     lhsT=bt[1][:, e, 0, :].bitcast(FP8X4),
                     lhsT_scale=bt[2][:, e, 0, :],
                     rhs=f_codes[c][:, 1, :].bitcast(FP8X4),
@@ -208,14 +215,14 @@ def tile_instrumentedlocmblock_pa_t_kernel(
                     start=True,
                     stop=True,
                 )
-                bu_t[c].append(bank)
+                bu_t[c].append(bank[:, e % share, :])
 
         def undamped_acceleration(c):
             accel_t[c] = work.tile([P, EVEN_ODD, states(c)], F32, name="accel_t", tag="accel_t", bufs=3)
             for e in range(EVEN_ODD):
                 nc.vector.scalar_tensor_tensor(
                     out=accel_t[c][:, e, :], in0=f_grouped[c][:, 0, :, e], scalar=neg_stiff_col[:, e:e + 1],
-                    in1=bu_t[c][e][:], op0=ALU.mult, op1=ALU.add,
+                    in1=bu_t[c][e], op0=ALU.mult, op1=ALU.add,
                 )
 
         def damping_net(c):
@@ -237,13 +244,13 @@ def tile_instrumentedlocmblock_pa_t_kernel(
 
         def damping_to_states(c):
             gamma = work.tile([P, CHUNK_TILES[c], MODES], F32, name="gamma", tag="gamma")
-            for s in range(CHUNK_TILES[c] // PAIR):
-                bank = scalar_bank([P, EVEN_ODD, PAIR, P])
-                for i in range(PAIR):
+            for pair in pairs(c):
+                bank = scalar_bank([P, EVEN_ODD, len(pair), P])
+                for i, t in enumerate(pair):
                     for e in range(EVEN_ODD):
-                        nc.tensor.transpose(bank[:, e, i, :], neg_tanh_t[c][:, e, tile_cols(s * PAIR + i)], ident[:])
+                        nc.tensor.transpose(bank[:, e, i, :], neg_tanh_t[c][:, e, tile_cols(t)], ident[:])
                 nc.scalar.activation(
-                    out=gamma[:, s * PAIR:(s + 1) * PAIR, :].rearrange("r i (p e) -> r (i p) e", e=EVEN_ODD),
+                    out=gamma[:, pair.start:pair.stop, :].rearrange("r i (p e) -> r (i p) e", e=EVEN_ODD),
                     in_=bank[:].rearrange("r e i p -> r (i p) e"),
                     func=ACT.Identity, bias=1.0, scale=-1.0,
                 )
@@ -257,37 +264,34 @@ def tile_instrumentedlocmblock_pa_t_kernel(
                 op0=ALU.add, op1=ALU.mult,
             )
 
-        def acceleration_to_states(c, pairs):
-            accel.setdefault(c, [])
-            for s in pairs:
-                bank = vector_bank([P, EVEN_ODD, PAIR, P])
-                for i in range(PAIR):
+        def acceleration_to_states(c):
+            accel[c] = []
+            for pair in pairs(c):
+                bank = vector_bank([P, EVEN_ODD, len(pair), P])
+                for i, t in enumerate(pair):
                     for e in range(EVEN_ODD):
-                        cols = tile_cols(s * PAIR + i)
                         nc.tensor.matmul(
-                            out=bank[:, e, i, :], lhsT=accel_t[c][:, e, cols], rhs=ident[:],
+                            out=bank[:, e, i, :], lhsT=accel_t[c][:, e, tile_cols(t)], rhs=ident[:],
                             is_transpose=True, start=True, stop=False,
                         )
                         nc.tensor.matmul(
-                            out=bank[:, e, i, :], lhsT=friction_t[c][:, e, cols], rhs=ident[:],
+                            out=bank[:, e, i, :], lhsT=friction_t[c][:, e, tile_cols(t)], rhs=ident[:],
                             is_transpose=True, start=False, stop=True,
                         )
                 accel[c].append(bank)
 
-        def step_z(c, pairs):
-            if c not in z_next:
-                z_next[c] = work.tile([P, CHUNK_TILES[c], MODES], F32, name="z_next", tag="z_next")
-            for s in pairs:
-                tiles = slice(s * PAIR, (s + 1) * PAIR)
+        def step_z(c):
+            z_next[c] = work.tile([P, CHUNK_TILES[c], MODES], F32, name="z_next", tag="z_next")
+            for pair, bank in zip(pairs(c), accel[c]):
+                tiles = slice(pair.start, pair.stop)
                 nc.vector.scalar_tensor_tensor(
                     out=z_next[c][:, tiles, :].rearrange("r i (p e) -> r (i p) e", e=EVEN_ODD),
-                    in0=accel[c][s][:].rearrange("r e i p -> r (i p) e"),
+                    in0=bank[:].rearrange("r e i p -> r (i p) e"),
                     scalar=dt_col[:, 0:1],
                     in1=z_sb[c][:, tiles, :].rearrange("r i (p e) -> r (i p) e", e=EVEN_ODD),
                     op0=ALU.mult, op1=ALU.add,
                 )
-            if CHUNK_TILES[c] // PAIR - 1 in pairs:
-                nc.sync.dma_start(out=z_next_rows[:, chunk_tiles(c), :], in_=z_next[c][:])
+            nc.sync.dma_start(out=z_next_rows[:, chunk_tiles(c), :], in_=z_next[c][:])
 
         def step_y(c):
             y_next = work.tile([P, CHUNK_TILES[c], MODES], F32, name="y_next", tag="y_next")
@@ -301,14 +305,22 @@ def tile_instrumentedlocmblock_pa_t_kernel(
         bt = weight_tiles("bt", EVEN_ODD, 1)
         w2 = weight_tiles("w2", EVEN_ODD, 1)
         w1_sb_blocks = w1_sb[:].rearrange("p h e k -> p (h e) k")
+        zeros = consts.tile([P, CLOCK_COLS], BF16)
+        nc.vector.memset(zeros[:], 0.0)
+
+        def keep_clock(n):
+            for k in range(n):
+                bank = vector_bank([P, CLOCK_COLS])
+                nc.tensor.matmul(out=bank[:], lhsT=zeros[:, 0:P], rhs=zeros[:], start=True, stop=True)
+        keep_clock(5)
         transpose_features(0)
         quantise_features(0)
         for b in range(HID_PLANES):
             regroup_weight(w1, w1_sb_blocks, [b], *(on_vector, on_scalar)[b % 2])
-        b1_bank = vector_bank([P, P])
+        b1_bank = scalar_bank([P, P])
         nc.tensor.transpose(b1_bank[:], b1_rows[:].bitcast(F32), ident[:])
         b1_col = consts.tile([P, HID_PLANES], F32)
-        nc.vector.tensor_copy(out=b1_col[:], in_=b1_bank[:, 0:2].bitcast(BF16))
+        nc.scalar.copy(out=b1_col[:], in_=b1_bank[:, 0:2].bitcast(BF16))
         for b in range(HID_PLANES):
             quantise_weight(w1, [b])
         transpose_features(1)
@@ -337,7 +349,7 @@ def tile_instrumentedlocmblock_pa_t_kernel(
                 nc.vector.tensor_copy(out=dt_col[:], in_=dt_bank[:, 0:1])
             c = i - 3
             if 0 <= c < N_CHUNKS:
-                acceleration_to_states(c, range(CHUNK_TILES[c] // PAIR))
+                acceleration_to_states(c)
             c = i - 2
             if 0 <= c < N_CHUNKS:
                 regroup_hidden(c)
@@ -355,7 +367,7 @@ def tile_instrumentedlocmblock_pa_t_kernel(
                 quantise_hidden(c)
             c = i - 3
             if 0 <= c < N_CHUNKS:
-                step_z(c, range(CHUNK_TILES[c] // PAIR))
+                step_z(c)
             c = i - 0
             if 2 <= c < N_CHUNKS:
                 quantise_features(c)

@@ -258,18 +258,19 @@ def tile_instrumentedlocmblock_pa_t_kernel(
 
         def friction(c):
             friction_t[c] = work.tile([P, EVEN_ODD, states(c)], F32, name="friction_t", tag="friction_t")
-            nc.vector.scalar_tensor_tensor(
-                out=friction_t[c][:], in0=neg_tanh_t[c][:], scalar=-1.0,
-                in1=f_grouped[c][:, 0, :, EVEN_ODD:2 * EVEN_ODD].rearrange("p r e -> p e r"),
-                op0=ALU.add, op1=ALU.mult,
-            )
+            for parities in [slice(0, EVEN_ODD)] if c < N_CHUNKS - 1 else [slice(e, e + 1) for e in range(EVEN_ODD)]:
+                nc.vector.scalar_tensor_tensor(
+                    out=friction_t[c][:, parities, :], in0=neg_tanh_t[c][:, parities, :], scalar=-1.0,
+                    in1=f_grouped[c][:, 0, :, EVEN_ODD + parities.start:EVEN_ODD + parities.stop].rearrange("p r e -> p e r"),
+                    op0=ALU.add, op1=ALU.mult,
+                )
 
         def acceleration_to_states(c):
             accel[c] = []
             for pair in pairs(c):
                 bank = vector_bank([P, EVEN_ODD, len(pair), P])
-                for i, t in enumerate(pair):
-                    for e in range(EVEN_ODD):
+                for e in range(EVEN_ODD):
+                    for i, t in enumerate(pair):
                         nc.tensor.matmul(
                             out=bank[:, e, i, :], lhsT=accel_t[c][:, e, tile_cols(t)], rhs=ident[:],
                             is_transpose=True, start=True, stop=False,
@@ -295,10 +296,14 @@ def tile_instrumentedlocmblock_pa_t_kernel(
 
         def step_y(c):
             y_next = work.tile([P, CHUNK_TILES[c], MODES], F32, name="y_next", tag="y_next")
-            nc.vector.scalar_tensor_tensor(
-                out=y_next[:], in0=z_next[c][:], scalar=dt_col[:, 0:1], in1=y_sb[c][:], op0=ALU.mult, op1=ALU.add,
-            )
-            nc.sync.dma_start(out=y_next_rows[:, chunk_tiles(c), :], in_=y_next[:])
+            pieces = [slice(0, CHUNK_TILES[c])] if c < N_CHUNKS - 1 else [slice(t, t + 1) for t in range(CHUNK_TILES[c])]
+            for tiles in pieces:
+                nc.vector.scalar_tensor_tensor(
+                    out=y_next[:, tiles, :], in0=z_next[c][:, tiles, :], scalar=dt_col[:, 0:1], in1=y_sb[c][:, tiles, :],
+                    op0=ALU.mult, op1=ALU.add,
+                )
+                rows = slice(FIRST_TILE[c] + tiles.start, FIRST_TILE[c] + tiles.stop)
+                nc.sync.dma_start(out=y_next_rows[:, rows, :], in_=y_next[:, tiles, :])
 
         on_scalar, on_vector = (scalar_bank, nc.scalar.copy), (vector_bank, nc.vector.tensor_copy)
         w1 = weight_tiles("w1", HID_PLANES, FEAT_PASSES)

import concourse.mybir as mybir
from concourse.masks import make_identity

F32 = mybir.dt.float32
BF16 = mybir.dt.bfloat16
U32 = mybir.dt.uint32
U8 = mybir.dt.uint8
FP8X4 = mybir.dt.float8_e4m3fn_x4
ACT = mybir.ActivationFunctionType
ALU = mybir.AluOpType

P = 128
PACK = 4
HALVES = 2
EVEN_ODD = 2
BATCH, MODES, DRIVE, HIDDEN = 4096, 256, 512, 512
FEATS = 2 * MODES + DRIVE
N_TILES = BATCH // P
CHUNK_TILES = (2, 2, 4, 4, 4, 4, 4, 4, 2, 2)
FIRST_TILE = tuple(sum(CHUNK_TILES[:c]) for c in range(len(CHUNK_TILES)))
N_CHUNKS = len(CHUNK_TILES)
MAX_TILES = max(CHUNK_TILES)
FEAT_PASSES = FEATS // (P * PACK)
HID_PLANES = HIDDEN // P
PAIR = 2
SCALAR_BANKS = 4
CLOCK_COLS = 512
BANK = 512
VECTOR_BANKS = 4

FLOPS = 2 * BATCH * FEATS * HIDDEN + 2 * BATCH * HIDDEN * MODES + 2 * BATCH * DRIVE * MODES


def tile_instrumentedlocmblock_pa_t_kernel(
    tc, y_tilde, z_tilde, u, dt, omega_sq, alpha_lambda, B_tilde, dmlp_w1, dmlp_b1, dmlp_w2, dmlp_b2,
    out_0, out_1, out_2,
):
    nc = tc.nc

    y_rows = y_tilde.rearrange("(p t) m -> p t m", t=N_TILES)
    z_rows = z_tilde.rearrange("(p t) m -> p t m", t=N_TILES)
    u_rows = u.rearrange("(p t) k -> p t k", t=N_TILES)
    z_next_rows = out_0.rearrange("(p t) m -> p t m", t=N_TILES)
    gamma_rows = out_1.rearrange("(p t) m -> p t m", t=N_TILES)
    y_next_rows = out_2.rearrange("(p t) m -> p t m", t=N_TILES)

    def chunk_tiles(c):
        return slice(FIRST_TILE[c], FIRST_TILE[c] + CHUNK_TILES[c])

    def states(c):
        return CHUNK_TILES[c] * P

    def pairs(c):
        return [range(t, min(t + PAIR, CHUNK_TILES[c])) for t in range(0, CHUNK_TILES[c], PAIR)]

    def tile_cols(t):
        return slice(t * P, (t + 1) * P)

    with tc.tile_pool(name="consts", bufs=1) as consts, \
            tc.tile_pool(name="inputs", bufs=N_CHUNKS) as inputs, \
            tc.tile_pool(name="work", bufs=2) as work, \
            tc.psum_pool(name="psum", bufs=1) as psum, \
            tc.manual_schedule():

        warm = consts.tile([P, 1], F32)
        nc.vector.memset(warm[:], 0.0)
        nc.scalar.activation(out=warm[:], in_=warm[:], func=ACT.Tanh)

        ident = consts.tile([P, P], F32)
        make_identity(nc, ident[:])

        y_sb, z_sb, u_sb = {}, {}, {}

        def load_chunk(c):
            y_sb[c] = inputs.tile([P, CHUNK_TILES[c], MODES], BF16, name="y_sb", tag="y%d" % CHUNK_TILES[c], bufs=CHUNK_TILES.count(CHUNK_TILES[c]))
            z_sb[c] = inputs.tile([P, CHUNK_TILES[c], MODES], BF16, name="z_sb", tag="z%d" % CHUNK_TILES[c], bufs=CHUNK_TILES.count(CHUNK_TILES[c]))
            u_sb[c] = inputs.tile([P, CHUNK_TILES[c], DRIVE], BF16, name="u_sb", tag="u%d" % CHUNK_TILES[c], bufs=CHUNK_TILES.count(CHUNK_TILES[c]))
            nc.sync.dma_start(out=y_sb[c][:], in_=y_rows[:, chunk_tiles(c), :])
            nc.sync.dma_start(out=z_sb[c][:], in_=z_rows[:, chunk_tiles(c), :])
            nc.sync.dma_start(out=u_sb[c][:], in_=u_rows[:, chunk_tiles(c), :])

        load_chunk(0)
        w1_sb = consts.tile([P, HALVES, EVEN_ODD, FEATS], BF16)
        w1_rows = dmlp_w1.rearrange("(h p e) k -> p h e k", h=HALVES, e=EVEN_ODD)
        for h in range(HALVES):
            nc.sync.dma_start(out=w1_sb[:, h], in_=w1_rows[:, h])
        b1_rows = consts.tile([P, EVEN_ODD * P], BF16)
        nc.vector.memset(b1_rows[:], 0.0)
        mode_rows = consts.tile([P, EVEN_ODD * P], BF16)
        nc.vector.memset(mode_rows[:], 0.0)
        dt_row = consts.tile([P, 2], BF16)
        nc.vector.memset(dt_row[:], 0.0)
        ones = consts.tile([P, 2], BF16)
        nc.vector.memset(ones[:], 1.0)
        bt_sb = consts.tile([P, EVEN_ODD, DRIVE], BF16)
        w2_sb = consts.tile([P, EVEN_ODD, HIDDEN], BF16)
        nc.sync.dma_start(out=b1_rows[0:2, :], in_=dmlp_b1.rearrange("(h w) -> h w", h=HALVES))
        load_chunk(1)
        nc.sync.dma_start(out=bt_sb[:], in_=B_tilde.rearrange("(p e) k -> p e k", e=EVEN_ODD))
        nc.sync.dma_start(out=w2_sb[:], in_=dmlp_w2.rearrange("(p e) k -> p e k", e=EVEN_ODD))
        load_chunk(2)
        for row, vector in enumerate((dmlp_b2, omega_sq, alpha_lambda)):
            nc.sync.dma_start(out=mode_rows[row:row + 1, :], in_=vector.rearrange("(o w) -> o w", o=1))
        nc.sync.dma_start(out=dt_row[0:1, 0:1], in_=dt.rearrange("(o w) -> o w", o=1))
        for c in range(3, N_CHUNKS):
            load_chunk(c)

        def scalar_bank(shape):
            return psum.tile(shape, F32, name="for_scalar", tag="for_scalar", bufs=SCALAR_BANKS)

        def vector_bank(shape):
            return psum.tile(shape, F32, name="for_vector", tag="for_vector", bufs=VECTOR_BANKS)

        def words_to_partitions(new_bank, copy, word_blocks, grouped_words):
            bank = new_bank([P, len(word_blocks), P])
            for q, block in enumerate(word_blocks):
                nc.tensor.transpose(bank[:, q, :], block, ident[:])
            copy(out=grouped_words, in_=bank[:].rearrange("p (g h) r -> p g r h", h=HALVES))

        def weight_tiles(name, blocks, passes):
            grouped = consts.tile([P, blocks, passes, P, PACK], BF16, name=name + "_grouped", align_bytes=64)
            codes = consts.tile([P, blocks, passes, P], U32, name=name + "_codes", align_bytes=64)
            scales = consts.tile([P, blocks, passes, P], U8, name=name + "_scales", align_bytes=64)
            return grouped, codes, scales

        def regroup_weight(tiles, rows_sb, blocks, new_bank, copy):
            word_blocks = []
            for b in blocks:
                words = rows_sb[:, b, :].bitcast(F32)
                word_blocks += [words[:, tile_cols(q)] for q in range(words.shape[1] // P)]
            words_to_partitions(
                new_bank, copy, word_blocks,
                tiles[0][:, blocks[0]:blocks[-1] + 1].rearrange("p b g r t -> p (b g) r t").bitcast(F32),
            )

        def quantise_weight(tiles, blocks):
            grouped, codes, scales = (x[:, blocks[0]:blocks[-1] + 1] for x in tiles)
            nc.vector.quantize_mx(
                out=codes.rearrange("p b g r -> p (b g r)").bitcast(FP8X4),
                scales=scales.rearrange("p b g r -> p (b g r)"),
                in_=grouped.rearrange("p b g r t -> p (b g r t)"),
            )

        f_grouped, f_codes, f_scales = {}, {}, {}
        h_planes, h_grouped, h_codes, h_scales = {}, {}, {}, {}
        bu_t, accel_t, neg_tanh_t, friction_t, accel, z_next = {}, {}, {}, {}, {}, {}

        def transpose_features(c, turns=((scalar_bank, nc.scalar.copy),)):
            f_grouped[c] = work.tile(
                [P, FEAT_PASSES, states(c), PACK], BF16, name="f_grouped", tag="f_grouped", align_bytes=64, bufs=4
            )
            for t in range(CHUNK_TILES[c]):
                u_words = u_sb[c][:, t, :].bitcast(F32)
                new_bank, copy = turns[t % len(turns)]
                words_to_partitions(
                    new_bank, copy,
                    [y_sb[c][:, t, :].bitcast(F32), z_sb[c][:, t, :].bitcast(F32), u_words[:, 0:P], u_words[:, P:2 * P]],
                    f_grouped[c][:].bitcast(F32)[:, :, tile_cols(t), :],
                )

        def quantise_features(c):
            f_codes[c] = work.tile([P, FEAT_PASSES, states(c)], U32, name="f_codes", tag="f_codes", align_bytes=64)
            f_scales[c] = work.tile([P, FEAT_PASSES, states(c)], U8, name="f_scales", tag="f_scales", align_bytes=64)
            nc.vector.quantize_mx(
                out=f_codes[c][:].rearrange("p g r -> p (g r)").bitcast(FP8X4),
                scales=f_scales[c][:].rearrange("p g r -> p (g r)"),
                in_=f_grouped[c][:].rearrange("p g r t -> p (g r t)"),
            )

        def hidden_layer(c, planes):
            if c not in h_planes:
                h_planes[c] = work.tile([P, HID_PLANES, states(c)], BF16, name="h_planes", tag="h_planes")
            for j in planes:
                acc = scalar_bank([P, states(c)])
                for g in range(FEAT_PASSES):
                    nc.tensor.matmul_mx(
                        out=acc[:],
                        lhsT=w1[1][:, j, g, :].bitcast(FP8X4),
                        lhsT_scale=w1[2][:, j, g, :],
                        rhs=f_codes[c][:, g, :].bitcast(FP8X4),
                        rhs_scale=f_scales[c][:, g, :],
                        start=(g == 0),
                        stop=(g == FEAT_PASSES - 1),
                    )
                nc.scalar.activation(out=h_planes[c][:, j, :], in_=acc[:], func=ACT.Tanh, bias=b1_col[:, j:j + 1], scale=1.0)

        def regroup_hidden(c):
            h_grouped[c] = work.tile([P, states(c), PACK], BF16, name="h_grouped", tag="h_grouped", align_bytes=64)
            nc.vector.tensor_copy(
                out=h_grouped[c][:].rearrange("p (c i) j -> p c j i", i=4),
                in_=h_planes[c][:].rearrange("p j (c i) -> p c j i", i=4),
            )

        def quantise_hidden(c):
            h_codes[c] = work.tile([P, states(c)], U32, name="h_codes", tag="h_codes", align_bytes=64)
            h_scales[c] = work.tile([P, states(c)], U8, name="h_scales", tag="h_scales", align_bytes=64)
            nc.vector.quantize_mx(
                out=h_codes[c][:].bitcast(FP8X4),
                scales=h_scales[c][:],
                in_=h_grouped[c][:].rearrange("p r j -> p (r j)"),
            )

        def drive_product(c):
            bu_t[c] = []
            share = min(EVEN_ODD, BANK // states(c))
            for e in range(EVEN_ODD):
                if e % share == 0:
                    bank = vector_bank([P, share, states(c)])
                nc.tensor.matmul_mx(
                    out=bank[:, e % share, :],
                    lhsT=bt[1][:, e, 0, :].bitcast(FP8X4),
                    lhsT_scale=bt[2][:, e, 0, :],
                    rhs=f_codes[c][:, 1, :].bitcast(FP8X4),
                    rhs_scale=f_scales[c][:, 1, :],
                    start=True,
                    stop=True,
                )
                bu_t[c].append(bank[:, e % share, :])

        def undamped_acceleration(c):
            accel_t[c] = work.tile([P, EVEN_ODD, states(c)], F32, name="accel_t", tag="accel_t", bufs=3)
            for e in range(EVEN_ODD):
                nc.vector.scalar_tensor_tensor(
                    out=accel_t[c][:, e, :], in0=f_grouped[c][:, 0, :, e], scalar=neg_stiff_col[:, e:e + 1],
                    in1=bu_t[c][e], op0=ALU.mult, op1=ALU.add,
                )

        def damping_net(c):
            neg_tanh_t[c] = work.tile([P, EVEN_ODD, states(c)], F32, name="neg_tanh_t", tag="neg_tanh_t")
            for e in range(EVEN_ODD):
                acc = scalar_bank([P, states(c)])
                nc.tensor.matmul_mx(
                    out=acc[:],
                    lhsT=w2[1][:, e, 0, :].bitcast(FP8X4),
                    lhsT_scale=w2[2][:, e, 0, :],
                    rhs=h_codes[c][:].bitcast(FP8X4),
                    rhs_scale=h_scales[c][:],
                    start=True,
                    stop=True,
                )
                nc.scalar.activation(
                    out=neg_tanh_t[c][:, e, :], in_=acc[:], func=ACT.Tanh, bias=neg_half_b2_col[:, e:e + 1], scale=-0.5
                )

        def damping_to_states(c):
            gamma = work.tile([P, CHUNK_TILES[c], MODES], F32, name="gamma", tag="gamma")
            for pair in pairs(c):
                bank = scalar_bank([P, EVEN_ODD, len(pair), P])
                for i, t in enumerate(pair):
                    for e in range(EVEN_ODD):
                        nc.tensor.transpose(bank[:, e, i, :], neg_tanh_t[c][:, e, tile_cols(t)], ident[:])
                nc.scalar.activation(
                    out=gamma[:, pair.start:pair.stop, :].rearrange("r i (p e) -> r (i p) e", e=EVEN_ODD),
                    in_=bank[:].rearrange("r e i p -> r (i p) e"),
                    func=ACT.Identity, bias=1.0, scale=-1.0,
                )
            nc.sync.dma_start(out=gamma_rows[:, chunk_tiles(c), :], in_=gamma[:])

        def friction(c):
            friction_t[c] = work.tile([P, EVEN_ODD, states(c)], F32, name="friction_t", tag="friction_t")
            for parities in [slice(0, EVEN_ODD)] if c < N_CHUNKS - 1 else [slice(e, e + 1) for e in range(EVEN_ODD)]:
                nc.vector.scalar_tensor_tensor(
                    out=friction_t[c][:, parities, :], in0=neg_tanh_t[c][:, parities, :], scalar=-1.0,
                    in1=f_grouped[c][:, 0, :, EVEN_ODD + parities.start:EVEN_ODD + parities.stop].rearrange("p r e -> p e r"),
                    op0=ALU.add, op1=ALU.mult,
                )

        def acceleration_to_states(c):
            accel[c] = []
            for pair in pairs(c):
                bank = vector_bank([P, EVEN_ODD, len(pair), P])
                for e in range(EVEN_ODD):
                    for i, t in enumerate(pair):
                        nc.tensor.matmul(
                            out=bank[:, e, i, :], lhsT=accel_t[c][:, e, tile_cols(t)], rhs=ident[:],
                            is_transpose=True, start=True, stop=False,
                        )
                        nc.tensor.matmul(
                            out=bank[:, e, i, :], lhsT=friction_t[c][:, e, tile_cols(t)], rhs=ident[:],
                            is_transpose=True, start=False, stop=True,
                        )
                accel[c].append(bank)

        def step_z(c):
            z_next[c] = work.tile([P, CHUNK_TILES[c], MODES], F32, name="z_next", tag="z_next")
            for pair, bank in zip(pairs(c), accel[c]):
                tiles = slice(pair.start, pair.stop)
                nc.vector.scalar_tensor_tensor(
                    out=z_next[c][:, tiles, :].rearrange("r i (p e) -> r (i p) e", e=EVEN_ODD),
                    in0=bank[:].rearrange("r e i p -> r (i p) e"),
                    scalar=dt_col[:, 0:1],
                    in1=z_sb[c][:, tiles, :].rearrange("r i (p e) -> r (i p) e", e=EVEN_ODD),
                    op0=ALU.mult, op1=ALU.add,
                )
            nc.sync.dma_start(out=z_next_rows[:, chunk_tiles(c), :], in_=z_next[c][:])

        def step_y(c):
            y_next = work.tile([P, CHUNK_TILES[c], MODES], F32, name="y_next", tag="y_next")
            pieces = [slice(0, CHUNK_TILES[c])] if c < N_CHUNKS - 1 else [slice(t, t + 1) for t in range(CHUNK_TILES[c])]
            for tiles in pieces:
                nc.vector.scalar_tensor_tensor(
                    out=y_next[:, tiles, :], in0=z_next[c][:, tiles, :], scalar=dt_col[:, 0:1], in1=y_sb[c][:, tiles, :],
                    op0=ALU.mult, op1=ALU.add,
                )
                rows = slice(FIRST_TILE[c] + tiles.start, FIRST_TILE[c] + tiles.stop)
                nc.sync.dma_start(out=y_next_rows[:, rows, :], in_=y_next[:, tiles, :])

        on_scalar, on_vector = (scalar_bank, nc.scalar.copy), (vector_bank, nc.vector.tensor_copy)
        w1 = weight_tiles("w1", HID_PLANES, FEAT_PASSES)
        bt = weight_tiles("bt", EVEN_ODD, 1)
        w2 = weight_tiles("w2", EVEN_ODD, 1)
        w1_sb_blocks = w1_sb[:].rearrange("p h e k -> p (h e) k")
        zeros = consts.tile([P, CLOCK_COLS], BF16)
        nc.vector.memset(zeros[:], 0.0)

        def keep_clock(n):
            for k in range(n):
                bank = vector_bank([P, CLOCK_COLS])
                nc.tensor.matmul(out=bank[:], lhsT=zeros[:, 0:P], rhs=zeros[:], start=True, stop=True)
        keep_clock(5)
        transpose_features(0)
        quantise_features(0)
        for b in range(HID_PLANES):
            regroup_weight(w1, w1_sb_blocks, [b], *(on_vector, on_scalar)[b % 2])
        b1_bank = scalar_bank([P, P])
        nc.tensor.transpose(b1_bank[:], b1_rows[:].bitcast(F32), ident[:])
        b1_col = consts.tile([P, HID_PLANES], F32)
        nc.scalar.copy(out=b1_col[:], in_=b1_bank[:, 0:2].bitcast(BF16))
        for b in range(HID_PLANES):
            quantise_weight(w1, [b])
        transpose_features(1)
        quantise_features(1)
        hidden_layer(0, range(HID_PLANES))
        regroup_weight(bt, bt_sb, [0, 1], *on_vector)
        regroup_weight(w2, w2_sb, [0, 1], *on_vector)
        quantise_weight(bt, [0, 1])
        quantise_weight(w2, [0, 1])
        for i in range(2, N_CHUNKS + 3):
            c = i - 0
            if 2 <= c < N_CHUNKS:
                transpose_features(c)
            if i == 2:
                mode_bank = vector_bank([P, P])
                nc.tensor.transpose(mode_bank[:], mode_rows[:].bitcast(F32), ident[:])
                mode_cols = consts.tile([P, 3 * EVEN_ODD], F32)
                nc.vector.tensor_copy(out=mode_cols[:], in_=mode_bank[:, 0:3].bitcast(BF16))
                neg_half_b2_col = consts.tile([P, EVEN_ODD], F32)
                nc.vector.tensor_scalar_mul(out=neg_half_b2_col[:], in0=mode_cols[:, 0:2], scalar1=-0.5)
                neg_stiff_col = consts.tile([P, EVEN_ODD], F32)
                nc.vector.tensor_tensor(out=neg_stiff_col[:], in0=mode_cols[:, 4:6], in1=mode_cols[:, 2:4], op=ALU.subtract)
                dt_bank = vector_bank([P, 2])
                nc.tensor.matmul(out=dt_bank[:], lhsT=dt_row[:, 0:1].to_broadcast([P, P]), rhs=ones[:], start=True, stop=True)
                dt_col = consts.tile([P, 1], F32)
                nc.vector.tensor_copy(out=dt_col[:], in_=dt_bank[:, 0:1])
            c = i - 3
            if 0 <= c < N_CHUNKS:
                acceleration_to_states(c)
            c = i - 2
            if 0 <= c < N_CHUNKS:
                regroup_hidden(c)
            c = i - 1
            if 2 <= c < N_CHUNKS:
                undamped_acceleration(c)
            c = i - 1
            if 1 <= c < N_CHUNKS:
                hidden_layer(c, (0, 1))
            if i == 2:
                drive_product(0)
                drive_product(1)
            c = i - 2
            if 0 <= c < N_CHUNKS:
                quantise_hidden(c)
            c = i - 3
            if 0 <= c < N_CHUNKS:
                step_z(c)
            c = i - 0
            if 2 <= c < N_CHUNKS:
                quantise_features(c)
            if i == 2:
                undamped_acceleration(0)
                undamped_acceleration(1)
            c = i - 2
            if 0 <= c < N_CHUNKS:
                damping_net(c)
            c = i - 1
            if 1 <= c < N_CHUNKS:
                hidden_layer(c, (2,))
            c = i - 1
            if 1 <= c < N_CHUNKS:
                hidden_layer(c, (3,))
            c = i - 3
            if 0 <= c < N_CHUNKS:
                step_y(c)
            c = i - 2
            if 0 <= c < N_CHUNKS:
                friction(c)
            c = i - 0
            if 2 <= c < N_CHUNKS:
                drive_product(c)
            c = i - 3
            if 0 <= c < N_CHUNKS:
                damping_to_states(c)
